import numpy as np
import ml_dtypes


def mxq(x, axis, fmt="e4m3"):
    dtype, down = {"e4m3": (ml_dtypes.float8_e4m3fn, 7), "e5m2": (ml_dtypes.float8_e5m2, 14)}[fmt]
    v = np.moveaxis(np.asarray(x, np.float32).astype(ml_dtypes.bfloat16).astype(np.float64), axis, -1)
    blocks = v.reshape(v.shape[:-1] + (-1, 32))
    amax = np.abs(blocks).max(-1, keepdims=True)
    byte = np.maximum(np.where(amax > 0, np.frexp(amax)[1] - 1 + 127, 0) - down, 1)
    scale = np.exp2(byte - 127.0)
    codes = (blocks / scale).astype(np.float32).astype(dtype).astype(np.float64)
    return np.moveaxis((codes * scale).reshape(v.shape), -1, axis)


WIDE = False


def mx_kscale(k):
    if not WIDE:
        return np.ones(k)
    levels = np.array([10, -10, 5, -5, 0])
    if k % 512:
        return np.exp2(np.random.permutation(np.resize(levels, k // 32))).repeat(32)
    a = np.empty((k // 512, 16))
    for p in range(k // 512):
        a[p, :8] = np.random.permutation(np.resize(levels, 8))
        for g in range(8):
            far = levels[np.abs(levels - a[p, g]) >= 10]
            a[p, g + 8] = far[np.random.randint(len(far))]
    return np.exp2(a.ravel()).repeat(32)


BF16 = ml_dtypes.bfloat16


def bf(x):
    return np.asarray(x, np.float32).astype(BF16)


def f64(x):
    return np.asarray(x).astype(np.float64)


B, I, H = 2048, 512, 256
EPS = 1e-5


def sigmoid(v):
    return 1.0 / (1.0 + np.exp(-v))


def _bn(v, gamma, beta):
    m = np.mean(v, axis=0)
    var = np.var(v, axis=0)
    return (v - m) * (gamma / np.sqrt(var + EPS)) + beta


def draw0():
    rn = np.random.standard_normal
    s = mx_kscale(I)
    return {"x": bf(rn((B, I)) * s),
            "c": bf(rn((B, H))),
            "h": bf(rn((B, H))),
            "w_ih": bf(rn((4 * H, I)) / np.sqrt(I) / s),
            "w_hh": bf(rn((4 * H, H)) / np.sqrt(H)),
            "b": bf(0.3 * rn(4 * H)),
            "g_ih": bf(1.0 + 0.1 * rn(4 * H)),
            "b_ih": bf(0.3 * rn(4 * H)),
            "g_hh": bf(1.0 + 0.1 * rn(4 * H)),
            "b_hh": bf(0.3 * rn(4 * H)),
            "g_c": bf(1.0 + 0.1 * rn(H)),
            "b_c": bf(0.3 * rn(H))}


def core(x, c, h, w_ih, w_hh, b, g_ih, b_ih, g_hh, b_hh, g_c, b_c):
    ih = mxq(f64(x), 1, "e4m3") @ mxq(f64(w_ih), 1, "e4m3").T
    hh = f64(h) @ f64(w_hh).T
    ih = _bn(ih, f64(g_ih), f64(b_ih))
    hh = _bn(hh, f64(g_hh), f64(b_hh))
    gates = ih + hh + f64(b)
    f, i, o, g = np.split(gates, 4, axis=1)
    f = sigmoid(f)
    i = sigmoid(i)
    o = sigmoid(o)
    g = np.tanh(g)
    c_next = f * f64(c) + i * g
    c_next = _bn(c_next, f64(g_c), f64(b_c))
    h_next = o * np.tanh(c_next)
    return (c_next, h_next)


def e4m3fn_bytes(y):
    return np.clip(np.asarray(y, np.float64), -448.0, 448.0).astype(np.float32).astype(ml_dtypes.float8_e4m3fn).view(np.uint8)


def e4m3fn_values(b):
    return np.asarray(b, np.uint8).view(ml_dtypes.float8_e4m3fn).astype(np.float64)


def setup_inputs():
    d = draw0()
    x0 = np.asarray(d['x']).astype(np.float64)
    s = (np.max(np.abs(x0), axis=(0,), keepdims=True) / 448.0).astype(np.float32)
    out = {}
    for k, v in d.items():
        if k == 'x':
            out['x_bytes'] = e4m3fn_bytes(x0 / s.astype(np.float64))
            out['x_scale'] = s
        else:
            out[k] = v
    return out


def reference(x_bytes, x_scale, c, h, w_ih, w_hh, b, g_ih, b_ih, g_hh, b_hh, g_c, b_c):
    return core(e4m3fn_values(x_bytes) * x_scale.astype(np.float64), c, h, w_ih, w_hh, b, g_ih, b_ih, g_hh, b_hh, g_c, b_c)

@@ -1,0 +1,469 @@
+from contextlib import ExitStack
+
+import concourse.mybir as mybir
+from concourse.masks import make_identity
+
+B, I, H = 2048, 512, 256
+EPS = 1e-5
+FLOPS = 2 * B * 4 * H * (I + H)
+
+F32 = mybir.dt.float32
+BF16 = mybir.dt.bfloat16
+U32 = mybir.dt.uint32
+U8 = mybir.dt.uint8
+FP8 = mybir.dt.float8_e4m3fn
+FP8X4 = mybir.dt.float8_e4m3fn_x4
+ALU = mybir.AluOpType
+ACT = mybir.ActivationFunctionType
+
+P = 128
+NB = B // P
+NQ = 4
+CW = 512
+NJ = 8
+ORDER = (0, 2, 6, 1, 3, 7, 4, 5)
+V_SHARE = (2, 2, 2, 2, 2, 2, 1, 1)
+ON_GPSIMD = ("fc0", "ig0", "fc1")
+WARM = 6
+PLAIN_DUMMIES = 10
+R_FILL = 0
+IH_BUFS = 3
+HH_BUFS = 3
+TP_BUFS = 2
+AHEAD = 2
+
+
+def tile_lstmcell_kernel(
+    tc, x_bytes, x_scale, c, h, w_ih, w_hh, b, g_ih, b_ih, g_hh, b_hh, g_c, b_c, out_0, out_1
+):
+    nc = tc.nc
+    with ExitStack() as ctx:
+        keep = ctx.enter_context(tc.tile_pool(name="keep", bufs=1))
+        work = ctx.enter_context(tc.tile_pool(name="work", bufs=2))
+        psum = ctx.enter_context(tc.psum_pool(name="psum", bufs=2))
+
+        def chunk(k, width=CW):
+            return slice(k * width, (k + 1) * width)
+
+        vra = keep.tile([P, P], BF16, name="vra")
+        vrb = keep.tile([P, P], BF16, name="vrb")
+        zero = keep.tile([P, CW], BF16, name="zero")
+        dm = keep.tile([P, 2], F32, name="dm")
+        nc.vector.memset(zero[:], 0.0)
+        nc.vector.memset(vra[:], 0.0)
+        nc.vector.memset(dm[:], 0.0)
+        nc.vector.memset(vrb[:], 0.0)
+
+        sc = keep.tile([P, I], F32, name="sc")
+        nc.sync.dma_start(out=sc[:], in_=x_scale.rearrange("o k -> (o k)").partition_broadcast(P))
+        nc.scalar.dma_start(out=vra[0:8, :], in_=g_hh.rearrange("(j m) -> j m", m=P))
+        xv = x_bytes.rearrange("(p n) k -> p n k", n=NB)
+        xbytes = []
+        for q in range(NQ):
+            xbt = keep.tile([P, 4, I], U8, name="xbytes%d" % q)
+            xbytes.append(xbt)
+        nc.sync.dma_start(out=xbytes[0][:], in_=xv[:, 0:4, :])
+        wh = keep.tile([P, NJ, H], BF16, name="wh")
+        nc.scalar.dma_start(out=wh[:], in_=w_hh.rearrange("(j m) k -> m j k", m=P))
+        hr = keep.tile([P, NB, H], BF16, name="hr")
+        hv = h.rearrange("(p n) k -> p n k", n=NB)
+        nc.sync.dma_start(out=xbytes[1][:], in_=xv[:, 4:8, :])
+        wi = keep.tile([P, NJ, I], BF16, name="wi")
+        wiv = w_ih.rearrange("(j m) k -> m j k", m=P)
+        nc.sync.dma_start(out=wi[:, 0:4, :], in_=wiv[:, 0:4, :])
+        nc.scalar.dma_start(out=hr[:, 0:8, :], in_=hv[:, 0:8, :])
+        nc.sync.dma_start(out=xbytes[2][:], in_=xv[:, 8:12, :])
+        nc.sync.dma_start(out=hr[:, 8:16, :], in_=hv[:, 8:16, :])
+        nc.sync.dma_start(out=xbytes[3][:], in_=xv[:, 12:16, :])
+        nc.sync.dma_start(out=wi[:, 4:8, :], in_=wiv[:, 4:8, :])
+        row = 0
+        for vec in (b, g_ih, b_ih, b_hh, g_c, b_c):
+            rows = vec.shape[0] // P
+            nc.sync.dma_start(out=vrb[row : row + rows, :], in_=vec.rearrange("(j m) -> j m", m=P))
+            row += rows
+        NV = row
+        cr = keep.tile([P, NB, H], BF16, name="cr")
+        cv = c.rearrange("(p n) k -> p n k", n=NB)
+        for half in range(2):
+            nc.sync.dma_start(out=cr[:, 8 * half : 8 * half + 8, :], in_=cv[:, 8 * half : 8 * half + 8, :])
+
+        nc.scalar.activation(out=dm[:, 1:2], in_=dm[:, 0:1], func=ACT.Sigmoid)
+        identb = keep.tile([P, P], BF16, name="identb")
+        make_identity(nc, identb[:])
+        warm = psum.tile([P, CW], F32, tag="tp", bufs=TP_BUFS, name="warm")
+        state = {"plain": 0, "mx": False}
+
+        def keep_warm(bank, n=R_FILL):
+            for i in range(n):
+                if state["mx"]:
+                    nc.tensor.matmul_mx(
+                        out=bank, lhsT=wq[:, 0:P].bitcast(FP8X4), lhsT_scale=ws[:, 0:P],
+                        rhs=wq[:, 0:CW].bitcast(FP8X4), rhs_scale=ws[:, 0:CW], start=True, stop=True,
+                    )
+                elif state["plain"] < PLAIN_DUMMIES:
+                    nc.tensor.matmul(out=bank, lhsT=identb[:], rhs=zero[:], start=True, stop=True)
+                    state["plain"] += 1
+
+        keep_warm(warm[:], WARM)
+        identf = keep.tile([P, P], F32, name="identf")
+        make_identity(nc, identf[:])
+        expo = keep.tile([P, 24], F32, name="expo")
+        nc.gpsimd.memset(expo[:, 0:8], -1.0)
+        nc.gpsimd.memset(expo[:, 8:16], -0.5)
+        nc.gpsimd.memset(expo[:, 16:24], 1.0)
+        mh = expo[:, 8:9]
+
+        pca = keep.tile([P, 8], F32, name="pca")
+        pcb = keep.tile([P, NV], F32, name="pcb")
+        v_g2 = pca[:, 0:8]
+        v_b, v_g1, v_b1, v_b2 = [pcb[:, 8 * i : 8 * i + 8] for i in range(4)]
+        v_gc, v_bc = pcb[:, 32:34], pcb[:, 34:36]
+        gc = keep.tile([P, 3, 8], F32, name="gc")
+        g2sq, igb, bsum = [gc[:, i, :] for i in range(3)]
+        gw = keep.tile([P, NJ + 2, 16], F32, name="gw")
+        nc.gpsimd.tensor_tensor(out=gw[:, 0, 15:16], in0=expo[:, 16:17], in1=mh, op=ALU.pow)
+
+        def vec_turn(src, dst, n):
+            pcp = psum.tile([P, P], BF16, tag="tp", bufs=TP_BUFS, name="pcp")
+            nc.tensor.transpose(pcp[:], src[:], identb[:])
+            nc.scalar.copy(out=dst[:], in_=pcp[:, 0:n])
+
+        def g2_consts():
+            nc.gpsimd.tensor_tensor(out=g2sq, in0=v_g2, in1=v_g2, op=ALU.mult)
+            nc.gpsimd.tensor_scalar(out=g2sq, in0=g2sq, scalar1=1e-30, scalar2=float(B), op0=ALU.max, op1=ALU.mult)
+            nc.gpsimd.tensor_tensor(out=igb, in0=g2sq, in1=expo[:, 0:8], op=ALU.pow)
+
+        def vec_consts():
+            nc.gpsimd.tensor_tensor(out=bsum, in0=v_b, in1=v_b1, op=ALU.add)
+            nc.gpsimd.tensor_tensor(out=bsum, in0=bsum, in1=v_b2, op=ALU.add)
+            nc.gpsimd.tensor_scalar(
+                out=gw[:, 0:NJ, 7], in0=v_g1, scalar1=-1.0, scalar2=0.0, op0=ALU.mult, op1=ALU.add
+            )
+            nc.gpsimd.tensor_scalar(
+                out=gw[:, NJ : NJ + 2, 6], in0=v_gc, scalar1=1.0, scalar2=0.0, op0=ALU.mult, op1=ALU.add
+            )
+            nc.gpsimd.tensor_scalar(
+                out=gw[:, NJ : NJ + 2, 7], in0=v_gc, scalar1=-1.0, scalar2=0.0, op0=ALU.mult, op1=ALU.add
+            )
+
+        whT = keep.tile([P, 2, NJ * P], BF16, name="whT")
+        hT = keep.tile([P, 2, B], BF16, name="hT")
+        cT = keep.tile([P, 2, B], BF16, name="cT")
+
+        def turn_bf16(src, dst, q, tag):
+            tp = psum.tile([P, 2, 4, P], BF16, tag=tag, bufs=(HH_BUFS if tag == "hh" else TP_BUFS), name="tb")
+            for e in range(2):
+                for a in range(4):
+                    nc.tensor.transpose(tp[:, e, a, :], src[:, 4 * q + a, e * P : (e + 1) * P], identb[:])
+            nc.scalar.copy(out=dst[:, :, chunk(q)], in_=tp[:].rearrange("k e a m -> k e (a m)"))
+
+        xq = keep.tile([P, B], U32, name="xq", align_bytes=64)
+        xs = keep.tile([P, B], U8, name="xs", align_bytes=64)
+        wq = keep.tile([P, NJ * P], U32, name="wq", align_bytes=64)
+        ws = keep.tile([P, NJ * P], U8, name="ws", align_bytes=64)
+        xbs, xgs, wgs = {}, {}, {}
+
+        def x_product(q):
+            xb = work.tile([P, 4, I], BF16, tag="xb", bufs=4, name="xb")
+            for a in range(4):
+                nc.vector.tensor_tensor(
+                    out=xb[:, a, :], in0=xbytes[q][:, a, :].bitcast(FP8), in1=sc[:], op=ALU.mult
+                )
+            xbs[q] = xb
+
+        def turn_words(rows2, dst_words, tag="ih"):
+            tw = psum.tile([P, 2, 2, P], F32, tag=tag, bufs=(IH_BUFS if tag == "ih" else TP_BUFS), name="tw")
+            keep_warm(tw[:].rearrange("k a u m -> k (a u m)"))
+            for a in range(2):
+                words = rows2[a].bitcast(F32)
+                for u in range(2):
+                    nc.tensor.transpose(tw[:, a, u, :], words[:, u : I // 2 : 2], identf[:])
+            nc.scalar.copy(out=dst_words, in_=tw[:].rearrange("k a u m -> k a m u"))
+
+        def x_turn(q):
+            xg = work.tile([P, CW, 4], BF16, tag="xg", bufs=4, name="xg", align_bytes=64)
+            xgw = xg[:].rearrange("k c t -> k (c t)").bitcast(F32).rearrange("k (a m u) -> k a m u", a=4, u=2)
+            for half in range(2):
+                turn_words(
+                    [xbs[q][:, 2 * half + a, :] for a in range(2)], xgw[:, 2 * half : 2 * half + 2, :, :]
+                )
+            xgs[q] = xg
+
+        def x_quant(q):
+            nc.vector.quantize_mx(
+                out=xq[:, chunk(q)].bitcast(FP8X4), scales=xs[:, chunk(q)],
+                in_=xgs[q][:].rearrange("k c t -> k (c t)"),
+            )
+
+        def w_turn(pr, tag="ih"):
+            wg = work.tile([P, 2 * P, 4], BF16, tag="wg", name="wg", align_bytes=64)
+            wgw = wg[:].rearrange("k c t -> k (c t)").bitcast(F32).rearrange("k (a m u) -> k a m u", a=2, u=2)
+            turn_words([wi[:, 2 * pr + a, :] for a in range(2)], wgw, tag)
+            wgs[pr] = wg
+
+        def w_quant(pr):
+            cols = slice(pr * 2 * P, (pr + 1) * 2 * P)
+            nc.vector.quantize_mx(
+                out=wq[:, cols].bitcast(FP8X4), scales=ws[:, cols],
+                in_=wgs[pr][:].rearrange("k c t -> k (c t)"),
+            )
+
+        gt = []
+        for j in range(NJ):
+            gtile = keep.tile([P, B], F32, name="gt%d" % j)
+            gt.append(gtile)
+        sy = keep.tile([P, NJ, 4], F32, name="sy")
+        qy = keep.tile([P, NJ], F32, name="qy")
+        mv = keep.tile([P, NJ + 2, 2], F32, name="mv")
+        ihp, sts = {}, {}
+        W2 = 2 * CW
+
+        def col(j, i):
+            return gw[:, j, i : i + 1]
+
+        def hh_bank(j, k, on_vector):
+            hp = psum.tile([P, CW], F32, tag="hh", bufs=HH_BUFS, name="hp")
+            keep_warm(hp[:])
+            for e in range(2):
+                nc.tensor.matmul(
+                    out=hp[:], lhsT=whT[:, e, j * P : (j + 1) * P], rhs=hT[:, e, chunk(k)],
+                    start=(e == 0), stop=(e == 1),
+                )
+            if on_vector:
+                nc.vector.tensor_scalar(
+                    out=gt[j][:, chunk(k)], in0=hp[:], scalar1=v_g2[:, j : j + 1], scalar2=None,
+                    op0=ALU.mult, op1=ALU.add, accum_out=sy[:, j, k : k + 1],
+                )
+            else:
+                nc.scalar.activation(
+                    out=gt[j][:, chunk(k)], in_=hp[:], func=ACT.Identity, scale=v_g2[:, j : j + 1],
+                    accum_out=sy[:, j, k : k + 1],
+                )
+
+        def hh_stats(j):
+            nc.gpsimd.tensor_tensor(out=gw[:, j, 0:2], in0=sy[:, j, 0:2], in1=sy[:, j, 2:4], op=ALU.add)
+            nc.gpsimd.tensor_scalar(
+                out=col(j, 2), in0=col(j, 0), scalar1=col(j, 1), scalar2=-1.0 / B, op0=ALU.add, op1=ALU.mult
+            )
+            junk = work.tile([P, B], BF16, tag="junk", name="junk")
+            nc.scalar.activation(
+                out=junk[:], in_=gt[j][:], func=ACT.Square, bias=col(j, 2), accum_out=qy[:, j : j + 1]
+            )
+            nc.gpsimd.tensor_scalar(
+                out=col(j, 3), in0=qy[:, j : j + 1], scalar1=igb[:, j : j + 1], scalar2=EPS,
+                op0=ALU.mult, op1=ALU.add,
+            )
+            nc.gpsimd.tensor_tensor(out=col(j, 4), in0=col(j, 3), in1=mh, op=ALU.pow)
+            nc.gpsimd.tensor_scalar(
+                out=col(j, 6), in0=col(j, 3), scalar1=col(j, 4), scalar2=v_g1[:, j : j + 1],
+                op0=ALU.mult, op1=ALU.mult,
+            )
+            nc.gpsimd.tensor_scalar(
+                out=col(j, 12), in0=col(j, 2), scalar1=col(j, 4), scalar2=bsum[:, j : j + 1],
+                op0=ALU.mult, op1=ALU.add,
+            )
+
+        def hh_stage(t):
+            for k in range(NQ):
+                hh_bank(ORDER[t], k, k < V_SHARE[t])
+            hh_stats(ORDER[t])
+
+        def norm_scalars(slot, beta):
+            nc.gpsimd.tensor_scalar(
+                out=col(slot, 5), in0=mv[:, slot, 1:2], scalar1=1.0, scalar2=EPS, op0=ALU.mult, op1=ALU.add
+            )
+            nc.gpsimd.tensor_tensor(out=col(slot, 8), in0=col(slot, 5), in1=mh, op=ALU.pow)
+            nc.gpsimd.tensor_scalar(
+                out=gw[:, slot, 9:11], in0=gw[:, slot, 6:8], scalar1=col(slot, 8), scalar2=0.0,
+                op0=ALU.mult, op1=ALU.add,
+            )
+            nc.gpsimd.tensor_scalar(
+                out=col(slot, 11), in0=mv[:, slot, 0:1], scalar1=col(slot, 10), scalar2=beta,
+                op0=ALU.mult, op1=ALU.add,
+            )
+
+        def ih_mm(j, k):
+            ip = psum.tile([P, CW], F32, tag="ih", bufs=IH_BUFS, name="ip")
+            keep_warm(ip[:])
+            nc.tensor.matmul_mx(
+                out=ip[:],
+                lhsT=wq[:, j * P : (j + 1) * P].bitcast(FP8X4), lhsT_scale=ws[:, j * P : (j + 1) * P],
+                rhs=xq[:, chunk(k)].bitcast(FP8X4), rhs_scale=xs[:, chunk(k)],
+                start=True, stop=True,
+            )
+            ihp[(j, k)] = ip
+
+        def ih_stats(j):
+            st = work.tile([P, NQ, 6], F32, tag="st", bufs=4, name="st")
+            for k in range(NQ):
+                ih_mm(j, k)
+                nc.vector.bn_stats(out=st[:, k, :], in_=ihp[(j, k)][:])
+            nc.vector.bn_aggr(out=mv[:, j, :], in_=st[:].rearrange("p a s -> p (a s)"))
+            norm_scalars(j, col(j, 12))
+
+        def combine(j, k):
+            ih_mm(j, k)
+            nc.vector.scalar_tensor_tensor(
+                out=gt[j][:, chunk(k)], in0=ihp[(j, k)][:], scalar=col(j, 9), in1=gt[j][:, chunk(k)],
+                op0=ALU.mult, op1=ALU.add,
+            )
+
+        def activate(j, half):
+            nc.scalar.activation(
+                out=gt[j][:, chunk(half, W2)], in_=gt[j][:, chunk(half, W2)],
+                func=(ACT.Tanh if j >= 6 else ACT.Sigmoid), scale=col(j, 4), bias=col(j, 11),
+            )
+
+        o0v = out_0.rearrange("(p n) c -> p n c", n=NB)
+        o1v = out_1.rearrange("(p n) c -> p n c", n=NB)
+
+        def store_turned(src, k, hd, outv, on_vector, tag="tp"):
+            pt = psum.tile([P, 4, P], F32, tag=tag, bufs=(IH_BUFS if tag == "ih" else TP_BUFS), name="pt")
+            keep_warm(pt[:].rearrange("p a m -> p (a m)"))
+            for a in range(4):
+                nc.tensor.transpose(pt[:, a, :], src[:, k * CW + a * P : k * CW + (a + 1) * P], identf[:])
+            sg = work.tile([P, 4, P], F32, tag="sg", bufs=8, name="sg")
+            if on_vector:
+                nc.vector.tensor_copy(out=sg[:], in_=pt[:])
+            else:
+                nc.scalar.copy(out=sg[:], in_=pt[:])
+            nc.sync.dma_start(out=outv[:, 4 * k : 4 * k + 4, hd * P : (hd + 1) * P], in_=sg[:])
+
+        def eng(what, hd):
+            return nc.gpsimd if (what + str(hd)) in ON_GPSIMD else nc.vector
+
+        def mul_fc(hd, half):
+            cs = chunk(half, W2)
+            eng("fc", hd).tensor_tensor(out=gt[hd][:, cs], in0=gt[hd][:, cs], in1=cT[:, hd, cs], op=ALU.mult)
+
+        def mul_ig(hd, half):
+            cs = chunk(half, W2)
+            eng("ig", hd).tensor_tensor(
+                out=gt[2 + hd][:, cs], in0=gt[2 + hd][:, cs], in1=gt[6 + hd][:, cs], op=ALU.mult
+            )
+
+        def add_c(hd, half):
+            cs = chunk(half, W2)
+            if half == 0:
+                st3 = work.tile([P, NQ, 6], F32, tag="st", bufs=4, name="st3")
+                sts[hd] = st3
+            eng("add", hd).tensor_tensor(out=gt[hd][:, cs], in0=gt[hd][:, cs], in1=gt[2 + hd][:, cs], op=ALU.add)
+            for k in (2 * half, 2 * half + 1):
+                nc.vector.bn_stats(out=sts[hd][:, k, :], in_=gt[hd][:, chunk(k)])
+
+        def c_scalars(hd):
+            s = NJ + hd
+            nc.vector.bn_aggr(out=mv[:, s, :], in_=sts[hd][:].rearrange("p a s -> p (a s)"))
+            norm_scalars(s, v_bc[:, hd : hd + 1])
+
+        def c_next(hd, half):
+            s = NJ + hd
+            cs = chunk(half, W2)
+            eng("cn", hd).tensor_scalar(
+                out=gt[2 + hd][:, cs], in0=gt[hd][:, cs], scalar1=col(s, 9), scalar2=col(s, 11),
+                op0=ALU.mult, op1=ALU.add,
+            )
+
+        def tanh_c(hd, half):
+            s = NJ + hd
+            cs = chunk(half, W2)
+            nc.scalar.activation(
+                out=gt[6 + hd][:, cs], in_=gt[hd][:, cs], func=ACT.Tanh, scale=col(s, 9), bias=col(s, 11)
+            )
+
+        def mul_oh(hd, k, width):
+            cs = chunk(k, width)
+            nc.vector.tensor_tensor(out=gt[4 + hd][:, cs], in0=gt[4 + hd][:, cs], in1=gt[6 + hd][:, cs], op=ALU.mult)
+
+        x_product(0)
+        turn_bf16(wh, whT, 0, "hh")
+        turn_bf16(wh, whT, 1, "hh")
+        vec_turn(vra, pca, 8)
+        g2_consts()
+        turn_bf16(hr, hT, 0, "hh")
+        turn_bf16(hr, hT, 1, "hh")
+        x_product(1)
+        x_turn(0)
+        turn_bf16(hr, hT, 2, "hh")
+        turn_bf16(hr, hT, 3, "hh")
+        vec_turn(vrb, pcb, NV)
+        vec_consts()
+        hh_stage(0)
+        x_product(2)
+        x_turn(1)
+        w_turn(0)
+        w_turn(1)
+        x_product(3)
+        x_turn(2)
+        w_quant(0)
+        w_quant(1)
+        state["mx"] = True
+        x_quant(0)
+        x_quant(1)
+        x_turn(3)
+        x_quant(2)
+        x_quant(3)
+        ih_stats(ORDER[0])
+        for t in range(1, AHEAD):
+            hh_stage(t)
+            ih_stats(ORDER[t])
+
+        def both(fn, hd):
+            fn(hd, 0)
+            fn(hd, 1)
+
+        def fill_first(t):
+            if t == 0:
+                w_turn(3, "tp")
+                w_quant(3)
+                turn_bf16(cr, cT, 0, "tp")
+                turn_bf16(cr, cT, 1, "tp")
+            if t == 1:
+                turn_bf16(cr, cT, 2, "tp")
+                turn_bf16(cr, cT, 3, "tp")
+
+        def fill_last(t):
+            if t == 1:
+                mul_fc(0, 0)
+            if t == 2:
+                mul_fc(0, 1)
+                w_turn(2, "tp")
+                w_quant(2)
+            if t == 3:
+                both(mul_ig, 0)
+            if t == 4:
+                both(add_c, 0)
+                c_scalars(0)
+            if t == 5:
+                both(mul_fc, 1)
+                both(c_next, 0)
+                both(tanh_c, 0)
+                for k in range(NQ):
+                    store_turned(gt[2], k, 0, o0v, False)
+            if t == 6:
+                both(mul_ig, 1)
+                both(add_c, 1)
+                c_scalars(1)
+            if t == 7:
+                mul_oh(0, 0, W2)
+                mul_oh(0, 1, W2)
+                both(c_next, 1)
+                both(tanh_c, 1)
+                for k in range(NQ):
+                    store_turned(gt[4], k, 0, o1v, False)
+                    store_turned(gt[3], k, 1, o0v, False)
+
+        for t in range(NJ):
+            j = ORDER[t]
+            fill_first(t)
+            fill_last(t)
+            for k in range(NQ):
+                combine(j, k)
+                if k % 2 == 1:
+                    activate(j, k // 2)
+            if t + AHEAD < NJ:
+                hh_stage(t + AHEAD)
+                ih_stats(ORDER[t + AHEAD])
+        for k in range(NQ):
+            mul_oh(1, k, CW)
+            store_turned(gt[5], k, 1, o1v, k >= 2, "ih")

@@ -41,6 +41,7 @@ def tile_lstmcell_kernel(
         keep = ctx.enter_context(tc.tile_pool(name="keep", bufs=1))
         work = ctx.enter_context(tc.tile_pool(name="work", bufs=2))
         psum = ctx.enter_context(tc.psum_pool(name="psum", bufs=2))
+        ctx.enter_context(tc.manual_schedule())
 
         def chunk(k, width=CW):
             return slice(k * width, (k + 1) * width)
@@ -56,7 +57,6 @@ def tile_lstmcell_kernel(
 
         sc = keep.tile([P, I], F32, name="sc")
         nc.sync.dma_start(out=sc[:], in_=x_scale.rearrange("o k -> (o k)").partition_broadcast(P))
-        nc.scalar.dma_start(out=vra[0:8, :], in_=g_hh.rearrange("(j m) -> j m", m=P))
         xv = x_bytes.rearrange("(p n) k -> p n k", n=NB)
         xbytes = []
         for q in range(NQ):
@@ -67,11 +67,12 @@ def tile_lstmcell_kernel(
         nc.scalar.dma_start(out=wh[:], in_=w_hh.rearrange("(j m) k -> m j k", m=P))
         hr = keep.tile([P, NB, H], BF16, name="hr")
         hv = h.rearrange("(p n) k -> p n k", n=NB)
+        nc.scalar.dma_start(out=hr[:, 0:8, :], in_=hv[:, 0:8, :])
+        nc.scalar.dma_start(out=vra[0:8, :], in_=g_hh.rearrange("(j m) -> j m", m=P))
         nc.sync.dma_start(out=xbytes[1][:], in_=xv[:, 4:8, :])
         wi = keep.tile([P, NJ, I], BF16, name="wi")
         wiv = w_ih.rearrange("(j m) k -> m j k", m=P)
         nc.sync.dma_start(out=wi[:, 0:4, :], in_=wiv[:, 0:4, :])
-        nc.scalar.dma_start(out=hr[:, 0:8, :], in_=hv[:, 0:8, :])
         nc.sync.dma_start(out=xbytes[2][:], in_=xv[:, 8:12, :])
         nc.sync.dma_start(out=hr[:, 8:16, :], in_=hv[:, 8:16, :])
         nc.sync.dma_start(out=xbytes[3][:], in_=xv[:, 12:16, :])
@@ -91,20 +92,8 @@ def tile_lstmcell_kernel(
         identb = keep.tile([P, P], BF16, name="identb")
         make_identity(nc, identb[:])
         warm = psum.tile([P, CW], F32, tag="tp", bufs=TP_BUFS, name="warm")
-        state = {"plain": 0, "mx": False}
-
-        def keep_warm(bank, n=R_FILL):
-            for i in range(n):
-                if state["mx"]:
-                    nc.tensor.matmul_mx(
-                        out=bank, lhsT=wq[:, 0:P].bitcast(FP8X4), lhsT_scale=ws[:, 0:P],
-                        rhs=wq[:, 0:CW].bitcast(FP8X4), rhs_scale=ws[:, 0:CW], start=True, stop=True,
-                    )
-                elif state["plain"] < PLAIN_DUMMIES:
-                    nc.tensor.matmul(out=bank, lhsT=identb[:], rhs=zero[:], start=True, stop=True)
-                    state["plain"] += 1
-
-        keep_warm(warm[:], WARM)
+        for i in range(WARM):
+            nc.tensor.matmul(out=warm[:], lhsT=identb[:], rhs=zero[:], start=True, stop=True)
         identf = keep.tile([P, P], F32, name="identf")
         make_identity(nc, identf[:])
         expo = keep.tile([P, 24], F32, name="expo")
@@ -123,91 +112,13 @@ def tile_lstmcell_kernel(
         gw = keep.tile([P, NJ + 2, 16], F32, name="gw")
         nc.gpsimd.tensor_tensor(out=gw[:, 0, 15:16], in0=expo[:, 16:17], in1=mh, op=ALU.pow)
 
-        def vec_turn(src, dst, n):
-            pcp = psum.tile([P, P], BF16, tag="tp", bufs=TP_BUFS, name="pcp")
-            nc.tensor.transpose(pcp[:], src[:], identb[:])
-            nc.scalar.copy(out=dst[:], in_=pcp[:, 0:n])
-
-        def g2_consts():
-            nc.gpsimd.tensor_tensor(out=g2sq, in0=v_g2, in1=v_g2, op=ALU.mult)
-            nc.gpsimd.tensor_scalar(out=g2sq, in0=g2sq, scalar1=1e-30, scalar2=float(B), op0=ALU.max, op1=ALU.mult)
-            nc.gpsimd.tensor_tensor(out=igb, in0=g2sq, in1=expo[:, 0:8], op=ALU.pow)
-
-        def vec_consts():
-            nc.gpsimd.tensor_tensor(out=bsum, in0=v_b, in1=v_b1, op=ALU.add)
-            nc.gpsimd.tensor_tensor(out=bsum, in0=bsum, in1=v_b2, op=ALU.add)
-            nc.gpsimd.tensor_scalar(
-                out=gw[:, 0:NJ, 7], in0=v_g1, scalar1=-1.0, scalar2=0.0, op0=ALU.mult, op1=ALU.add
-            )
-            nc.gpsimd.tensor_scalar(
-                out=gw[:, NJ : NJ + 2, 6], in0=v_gc, scalar1=1.0, scalar2=0.0, op0=ALU.mult, op1=ALU.add
-            )
-            nc.gpsimd.tensor_scalar(
-                out=gw[:, NJ : NJ + 2, 7], in0=v_gc, scalar1=-1.0, scalar2=0.0, op0=ALU.mult, op1=ALU.add
-            )
-
         whT = keep.tile([P, 2, NJ * P], BF16, name="whT")
         hT = keep.tile([P, 2, B], BF16, name="hT")
         cT = keep.tile([P, 2, B], BF16, name="cT")
-
-        def turn_bf16(src, dst, q, tag):
-            tp = psum.tile([P, 2, 4, P], BF16, tag=tag, bufs=(HH_BUFS if tag == "hh" else TP_BUFS), name="tb")
-            for e in range(2):
-                for a in range(4):
-                    nc.tensor.transpose(tp[:, e, a, :], src[:, 4 * q + a, e * P : (e + 1) * P], identb[:])
-            nc.scalar.copy(out=dst[:, :, chunk(q)], in_=tp[:].rearrange("k e a m -> k e (a m)"))
-
         xq = keep.tile([P, B], U32, name="xq", align_bytes=64)
         xs = keep.tile([P, B], U8, name="xs", align_bytes=64)
         wq = keep.tile([P, NJ * P], U32, name="wq", align_bytes=64)
         ws = keep.tile([P, NJ * P], U8, name="ws", align_bytes=64)
-        xbs, xgs, wgs = {}, {}, {}
-
-        def x_product(q):
-            xb = work.tile([P, 4, I], BF16, tag="xb", bufs=4, name="xb")
-            for a in range(4):
-                nc.vector.tensor_tensor(
-                    out=xb[:, a, :], in0=xbytes[q][:, a, :].bitcast(FP8), in1=sc[:], op=ALU.mult
-                )
-            xbs[q] = xb
-
-        def turn_words(rows2, dst_words, tag="ih"):
-            tw = psum.tile([P, 2, 2, P], F32, tag=tag, bufs=(IH_BUFS if tag == "ih" else TP_BUFS), name="tw")
-            keep_warm(tw[:].rearrange("k a u m -> k (a u m)"))
-            for a in range(2):
-                words = rows2[a].bitcast(F32)
-                for u in range(2):
-                    nc.tensor.transpose(tw[:, a, u, :], words[:, u : I // 2 : 2], identf[:])
-            nc.scalar.copy(out=dst_words, in_=tw[:].rearrange("k a u m -> k a m u"))
-
-        def x_turn(q):
-            xg = work.tile([P, CW, 4], BF16, tag="xg", bufs=4, name="xg", align_bytes=64)
-            xgw = xg[:].rearrange("k c t -> k (c t)").bitcast(F32).rearrange("k (a m u) -> k a m u", a=4, u=2)
-            for half in range(2):
-                turn_words(
-                    [xbs[q][:, 2 * half + a, :] for a in range(2)], xgw[:, 2 * half : 2 * half + 2, :, :]
-                )
-            xgs[q] = xg
-
-        def x_quant(q):
-            nc.vector.quantize_mx(
-                out=xq[:, chunk(q)].bitcast(FP8X4), scales=xs[:, chunk(q)],
-                in_=xgs[q][:].rearrange("k c t -> k (c t)"),
-            )
-
-        def w_turn(pr, tag="ih"):
-            wg = work.tile([P, 2 * P, 4], BF16, tag="wg", name="wg", align_bytes=64)
-            wgw = wg[:].rearrange("k c t -> k (c t)").bitcast(F32).rearrange("k (a m u) -> k a m u", a=2, u=2)
-            turn_words([wi[:, 2 * pr + a, :] for a in range(2)], wgw, tag)
-            wgs[pr] = wg
-
-        def w_quant(pr):
-            cols = slice(pr * 2 * P, (pr + 1) * 2 * P)
-            nc.vector.quantize_mx(
-                out=wq[:, cols].bitcast(FP8X4), scales=ws[:, cols],
-                in_=wgs[pr][:].rearrange("k c t -> k (c t)"),
-            )
-
         gt = []
         for j in range(NJ):
             gtile = keep.tile([P, B], F32, name="gt%d" % j)
@@ -215,255 +126,646 @@ def tile_lstmcell_kernel(
         sy = keep.tile([P, NJ, 4], F32, name="sy")
         qy = keep.tile([P, NJ], F32, name="qy")
         mv = keep.tile([P, NJ + 2, 2], F32, name="mv")
-        ihp, sts = {}, {}
+        o0v = out_0.rearrange("(p n) c -> p n c", n=NB)
+        o1v = out_1.rearrange("(p n) c -> p n c", n=NB)
         W2 = 2 * CW
+        ps, xbs, xgs, wgs, sts = {}, {}, {}, {}, {}
 
         def col(j, i):
             return gw[:, j, i : i + 1]
 
-        def hh_bank(j, k, on_vector):
-            hp = psum.tile([P, CW], F32, tag="hh", bufs=HH_BUFS, name="hp")
-            keep_warm(hp[:])
+        queues = {"pe": [], "v": [], "s": [], "g": []}
+        rings = {"ih": [], "hh": [], "tp": []}
+        BUFS = {"ih": IH_BUFS, "hh": HH_BUFS, "tp": TP_BUFS}
+
+        def put(q, name, needs, fn, *args):
+            queues[q].append((name, tuple(needs), fn, args))
+
+        def fill(tag, name, needs, fn, *args):
+            ring = rings[tag]
+            needs = tuple(needs)
+            if len(ring) >= BUFS[tag]:
+                needs = needs + (ring[len(ring) - BUFS[tag]],)
+            ring.append(("r",) + name)
+            put("pe", name, needs, fn, tag, name, *args)
+
+        def engine(q):
+            return {"v": nc.vector, "s": nc.scalar, "g": nc.gpsimd}[q]
+
+        def f_tb(tag, name, src, q):
+            t = psum.tile([P, 2, 4, P], BF16, tag=tag, bufs=BUFS[tag], name="tb")
+            ps[name] = t
+            for e in range(2):
+                for a in range(4):
+                    nc.tensor.transpose(t[:, e, a, :], src[:, 4 * q + a, e * P : (e + 1) * P], identb[:])
+
+        def r_tb(q_, name, dst, q):
+            src = ps[name][:].rearrange("k e a m -> k e (a m)")
+            if q_ == "v":
+                nc.vector.tensor_copy(out=dst[:, :, chunk(q)], in_=src)
+            else:
+                nc.scalar.copy(out=dst[:, :, chunk(q)], in_=src)
+
+        def f_vec(tag, name, src):
+            t = psum.tile([P, P], BF16, tag=tag, bufs=BUFS[tag], name="pcp")
+            ps[name] = t
+            nc.tensor.transpose(t[:], src[:], identb[:])
+
+        def r_vec(name, dst, n):
+            nc.scalar.copy(out=dst[:], in_=ps[name][:, 0:n])
+
+        def f_tw(tag, name, rows):
+            t = psum.tile([P, 2, 2, P], F32, tag=tag, bufs=BUFS[tag], name="tw")
+            ps[name] = t
+            for a in range(2):
+                words = rows(a).bitcast(F32)
+                for u in range(2):
+                    nc.tensor.transpose(t[:, a, u, :], words[:, u : I // 2 : 2], identf[:])
+
+        def r_tw(name, dst):
+            nc.scalar.copy(out=dst(), in_=ps[name][:].rearrange("k a u m -> k a m u"))
+
+        def s_xp(q, a):
+            if a == 0:
+                xb = work.tile([P, 4, I], BF16, tag="xb", bufs=4, name="xb")
+                xbs[q] = xb
+            nc.vector.tensor_tensor(out=xbs[q][:, a, :], in0=xbytes[q][:, a, :].bitcast(FP8), in1=sc[:], op=ALU.mult)
+
+        def x_dst(q, half):
+            if half == 0:
+                xg = work.tile([P, CW, 4], BF16, tag="xg", bufs=4, name="xg", align_bytes=64)
+                xgs[q] = xg
+            v = xgs[q][:].rearrange("k c t -> k (c t)").bitcast(F32).rearrange("k (a m u) -> k a m u", a=4, u=2)
+            return v[:, 2 * half : 2 * half + 2, :, :]
+
+        def w_dst(pr):
+            wg = work.tile([P, 2 * P, 4], BF16, tag="wg", bufs=4, name="wg", align_bytes=64)
+            wgs[pr] = wg
+            return wg[:].rearrange("k c t -> k (c t)").bitcast(F32).rearrange("k (a m u) -> k a m u", a=2, u=2)
+
+        def s_xq(q):
+            nc.vector.quantize_mx(
+                out=xq[:, chunk(q)].bitcast(FP8X4), scales=xs[:, chunk(q)], in_=xgs[q][:].rearrange("k c t -> k (c t)")
+            )
+
+        def s_wq(pr):
+            cols = slice(pr * 2 * P, (pr + 1) * 2 * P)
+            nc.vector.quantize_mx(
+                out=wq[:, cols].bitcast(FP8X4), scales=ws[:, cols], in_=wgs[pr][:].rearrange("k c t -> k (c t)")
+            )
+
+        def s_g2c():
+            nc.gpsimd.tensor_tensor(out=g2sq, in0=v_g2, in1=v_g2, op=ALU.mult)
+            nc.gpsimd.tensor_scalar(out=g2sq, in0=g2sq, scalar1=1e-30, scalar2=float(B), op0=ALU.max, op1=ALU.mult)
+            nc.gpsimd.tensor_tensor(out=igb, in0=g2sq, in1=expo[:, 0:8], op=ALU.pow)
+
+        def s_vc():
+            nc.gpsimd.tensor_tensor(out=bsum, in0=v_b, in1=v_b1, op=ALU.add)
+            nc.gpsimd.tensor_tensor(out=bsum, in0=bsum, in1=v_b2, op=ALU.add)
+            nc.gpsimd.tensor_scalar(out=gw[:, 0:NJ, 7], in0=v_g1, scalar1=-1.0, scalar2=0.0, op0=ALU.mult, op1=ALU.add)
+            nc.gpsimd.tensor_scalar(
+                out=gw[:, NJ : NJ + 2, 6], in0=v_gc, scalar1=1.0, scalar2=0.0, op0=ALU.mult, op1=ALU.add
+            )
+            nc.gpsimd.tensor_scalar(
+                out=gw[:, NJ : NJ + 2, 7], in0=v_gc, scalar1=-1.0, scalar2=0.0, op0=ALU.mult, op1=ALU.add
+            )
+
+        def f_hh(tag, name, j, k):
+            t = psum.tile([P, CW], F32, tag=tag, bufs=BUFS[tag], name="hp")
+            ps[name] = t
             for e in range(2):
                 nc.tensor.matmul(
-                    out=hp[:], lhsT=whT[:, e, j * P : (j + 1) * P], rhs=hT[:, e, chunk(k)],
-                    start=(e == 0), stop=(e == 1),
+                    out=t[:], lhsT=whT[:, e, j * P : (j + 1) * P], rhs=hT[:, e, chunk(k)], start=(e == 0), stop=(e == 1)
                 )
-            if on_vector:
+
+        def r_hh(q_, name, j, k):
+            if q_ == "v":
                 nc.vector.tensor_scalar(
-                    out=gt[j][:, chunk(k)], in0=hp[:], scalar1=v_g2[:, j : j + 1], scalar2=None,
+                    out=gt[j][:, chunk(k)], in0=ps[name][:], scalar1=v_g2[:, j : j + 1], scalar2=None,
                     op0=ALU.mult, op1=ALU.add, accum_out=sy[:, j, k : k + 1],
                 )
             else:
                 nc.scalar.activation(
-                    out=gt[j][:, chunk(k)], in_=hp[:], func=ACT.Identity, scale=v_g2[:, j : j + 1],
+                    out=gt[j][:, chunk(k)], in_=ps[name][:], func=ACT.Identity, scale=v_g2[:, j : j + 1],
                     accum_out=sy[:, j, k : k + 1],
                 )
 
-        def hh_stats(j):
+        def s_g1(j):
             nc.gpsimd.tensor_tensor(out=gw[:, j, 0:2], in0=sy[:, j, 0:2], in1=sy[:, j, 2:4], op=ALU.add)
             nc.gpsimd.tensor_scalar(
                 out=col(j, 2), in0=col(j, 0), scalar1=col(j, 1), scalar2=-1.0 / B, op0=ALU.add, op1=ALU.mult
             )
+
+        def s_q(j):
             junk = work.tile([P, B], BF16, tag="junk", name="junk")
-            nc.scalar.activation(
-                out=junk[:], in_=gt[j][:], func=ACT.Square, bias=col(j, 2), accum_out=qy[:, j : j + 1]
-            )
+            nc.scalar.activation(out=junk[:], in_=gt[j][:], func=ACT.Square, bias=col(j, 2), accum_out=qy[:, j : j + 1])
+
+        def s_g2(j):
             nc.gpsimd.tensor_scalar(
-                out=col(j, 3), in0=qy[:, j : j + 1], scalar1=igb[:, j : j + 1], scalar2=EPS,
-                op0=ALU.mult, op1=ALU.add,
+                out=col(j, 3), in0=qy[:, j : j + 1], scalar1=igb[:, j : j + 1], scalar2=EPS, op0=ALU.mult, op1=ALU.add
             )
             nc.gpsimd.tensor_tensor(out=col(j, 4), in0=col(j, 3), in1=mh, op=ALU.pow)
             nc.gpsimd.tensor_scalar(
-                out=col(j, 6), in0=col(j, 3), scalar1=col(j, 4), scalar2=v_g1[:, j : j + 1],
-                op0=ALU.mult, op1=ALU.mult,
+                out=col(j, 6), in0=col(j, 3), scalar1=col(j, 4), scalar2=v_g1[:, j : j + 1], op0=ALU.mult, op1=ALU.mult
             )
             nc.gpsimd.tensor_scalar(
-                out=col(j, 12), in0=col(j, 2), scalar1=col(j, 4), scalar2=bsum[:, j : j + 1],
-                op0=ALU.mult, op1=ALU.add,
+                out=col(j, 12), in0=col(j, 2), scalar1=col(j, 4), scalar2=bsum[:, j : j + 1], op0=ALU.mult, op1=ALU.add
             )
 
-        def hh_stage(t):
-            for k in range(NQ):
-                hh_bank(ORDER[t], k, k < V_SHARE[t])
-            hh_stats(ORDER[t])
-
-        def norm_scalars(slot, beta):
+        def s_norm(slot, beta):
             nc.gpsimd.tensor_scalar(
                 out=col(slot, 5), in0=mv[:, slot, 1:2], scalar1=1.0, scalar2=EPS, op0=ALU.mult, op1=ALU.add
             )
             nc.gpsimd.tensor_tensor(out=col(slot, 8), in0=col(slot, 5), in1=mh, op=ALU.pow)
             nc.gpsimd.tensor_scalar(
-                out=gw[:, slot, 9:11], in0=gw[:, slot, 6:8], scalar1=col(slot, 8), scalar2=0.0,
-                op0=ALU.mult, op1=ALU.add,
+                out=gw[:, slot, 9:11], in0=gw[:, slot, 6:8], scalar1=col(slot, 8), scalar2=0.0, op0=ALU.mult, op1=ALU.add
             )
             nc.gpsimd.tensor_scalar(
-                out=col(slot, 11), in0=mv[:, slot, 0:1], scalar1=col(slot, 10), scalar2=beta,
-                op0=ALU.mult, op1=ALU.add,
+                out=col(slot, 11), in0=mv[:, slot, 0:1], scalar1=col(slot, 10), scalar2=beta, op0=ALU.mult, op1=ALU.add
             )
 
-        def ih_mm(j, k):
-            ip = psum.tile([P, CW], F32, tag="ih", bufs=IH_BUFS, name="ip")
-            keep_warm(ip[:])
+        def s_g23(ja, jb):
+            if jb is not None:
+                nc.gpsimd.tensor_scalar(
+                    out=col(jb, 3), in0=qy[:, jb : jb + 1], scalar1=igb[:, jb : jb + 1], scalar2=EPS, op0=ALU.mult, op1=ALU.add
+                )
+            if ja is not None:
+                nc.gpsimd.tensor_scalar(
+                    out=col(ja, 5), in0=mv[:, ja, 1:2], scalar1=1.0, scalar2=EPS, op0=ALU.mult, op1=ALU.add
+                )
+            if jb is not None:
+                nc.gpsimd.tensor_tensor(out=col(jb, 4), in0=col(jb, 3), in1=mh, op=ALU.pow)
+            if ja is not None:
+                nc.gpsimd.tensor_tensor(out=col(ja, 8), in0=col(ja, 5), in1=mh, op=ALU.pow)
+            if jb is not None:
+                nc.gpsimd.tensor_scalar(
+                    out=col(jb, 6), in0=col(jb, 3), scalar1=col(jb, 4), scalar2=v_g1[:, jb : jb + 1], op0=ALU.mult, op1=ALU.mult
+                )
+            if ja is not None:
+                nc.gpsimd.tensor_scalar(
+                    out=gw[:, ja, 9:11], in0=gw[:, ja, 6:8], scalar1=col(ja, 8), scalar2=0.0, op0=ALU.mult, op1=ALU.add
+                )
+            if jb is not None:
+                nc.gpsimd.tensor_scalar(
+                    out=col(jb, 12), in0=col(jb, 2), scalar1=col(jb, 4), scalar2=bsum[:, jb : jb + 1], op0=ALU.mult, op1=ALU.add
+                )
+            if ja is not None:
+                nc.gpsimd.tensor_scalar(
+                    out=col(ja, 11), in0=mv[:, ja, 0:1], scalar1=col(ja, 10), scalar2=col(ja, 12), op0=ALU.mult, op1=ALU.add
+                )
+
+        def f_mx(tag, name, j, k):
+            t = psum.tile([P, CW], F32, tag=tag, bufs=BUFS[tag], name="ip")
+            ps[name] = t
             nc.tensor.matmul_mx(
-                out=ip[:],
+                out=t[:],
                 lhsT=wq[:, j * P : (j + 1) * P].bitcast(FP8X4), lhsT_scale=ws[:, j * P : (j + 1) * P],
                 rhs=xq[:, chunk(k)].bitcast(FP8X4), rhs_scale=xs[:, chunk(k)],
                 start=True, stop=True,
             )
-            ihp[(j, k)] = ip
 
-        def ih_stats(j):
-            st = work.tile([P, NQ, 6], F32, tag="st", bufs=4, name="st")
-            for k in range(NQ):
-                ih_mm(j, k)
-                nc.vector.bn_stats(out=st[:, k, :], in_=ihp[(j, k)][:])
-            nc.vector.bn_aggr(out=mv[:, j, :], in_=st[:].rearrange("p a s -> p (a s)"))
-            norm_scalars(j, col(j, 12))
+        def r_bn(name, j, k):
+            if k == 0:
+                st = work.tile([P, NQ, 6], F32, tag="st", bufs=4, name="st")
+                sts[j] = st
+            nc.vector.bn_stats(out=sts[j][:, k, :], in_=ps[name][:])
 
-        def combine(j, k):
-            ih_mm(j, k)
+        def s_aggr(slot, key):
+            nc.vector.bn_aggr(out=mv[:, slot, :], in_=sts[key][:].rearrange("p a s -> p (a s)"))
+
+        def r_join(name, j, k):
             nc.vector.scalar_tensor_tensor(
-                out=gt[j][:, chunk(k)], in0=ihp[(j, k)][:], scalar=col(j, 9), in1=gt[j][:, chunk(k)],
+                out=gt[j][:, chunk(k)], in0=ps[name][:], scalar=col(j, 9), in1=gt[j][:, chunk(k)],
                 op0=ALU.mult, op1=ALU.add,
             )
 
-        def activate(j, half):
+        def s_act(j, half):
             nc.scalar.activation(
                 out=gt[j][:, chunk(half, W2)], in_=gt[j][:, chunk(half, W2)],
                 func=(ACT.Tanh if j >= 6 else ACT.Sigmoid), scale=col(j, 4), bias=col(j, 11),
             )
 
-        o0v = out_0.rearrange("(p n) c -> p n c", n=NB)
-        o1v = out_1.rearrange("(p n) c -> p n c", n=NB)
-
-        def store_turned(src, k, hd, outv, on_vector, tag="tp"):
-            pt = psum.tile([P, 4, P], F32, tag=tag, bufs=(IH_BUFS if tag == "ih" else TP_BUFS), name="pt")
-            keep_warm(pt[:].rearrange("p a m -> p (a m)"))
-            for a in range(4):
-                nc.tensor.transpose(pt[:, a, :], src[:, k * CW + a * P : k * CW + (a + 1) * P], identf[:])
-            sg = work.tile([P, 4, P], F32, tag="sg", bufs=8, name="sg")
-            if on_vector:
-                nc.vector.tensor_copy(out=sg[:], in_=pt[:])
-            else:
-                nc.scalar.copy(out=sg[:], in_=pt[:])
-            nc.sync.dma_start(out=outv[:, 4 * k : 4 * k + 4, hd * P : (hd + 1) * P], in_=sg[:])
-
-        def eng(what, hd):
-            return nc.gpsimd if (what + str(hd)) in ON_GPSIMD else nc.vector
-
-        def mul_fc(hd, half):
+        def s_fc(q_, hd, half):
             cs = chunk(half, W2)
-            eng("fc", hd).tensor_tensor(out=gt[hd][:, cs], in0=gt[hd][:, cs], in1=cT[:, hd, cs], op=ALU.mult)
+            engine(q_).tensor_tensor(out=gt[hd][:, cs], in0=gt[hd][:, cs], in1=cT[:, hd, cs], op=ALU.mult)
 
-        def mul_ig(hd, half):
+        def s_ig(q_, hd, half):
             cs = chunk(half, W2)
-            eng("ig", hd).tensor_tensor(
-                out=gt[2 + hd][:, cs], in0=gt[2 + hd][:, cs], in1=gt[6 + hd][:, cs], op=ALU.mult
-            )
+            engine(q_).tensor_tensor(out=gt[2 + hd][:, cs], in0=gt[2 + hd][:, cs], in1=gt[6 + hd][:, cs], op=ALU.mult)
 
-        def add_c(hd, half):
+        def s_add(hd, half):
             cs = chunk(half, W2)
             if half == 0:
                 st3 = work.tile([P, NQ, 6], F32, tag="st", bufs=4, name="st3")
-                sts[hd] = st3
-            eng("add", hd).tensor_tensor(out=gt[hd][:, cs], in0=gt[hd][:, cs], in1=gt[2 + hd][:, cs], op=ALU.add)
+                sts[NJ + hd] = st3
+            nc.vector.tensor_tensor(out=gt[hd][:, cs], in0=gt[hd][:, cs], in1=gt[2 + hd][:, cs], op=ALU.add)
             for k in (2 * half, 2 * half + 1):
-                nc.vector.bn_stats(out=sts[hd][:, k, :], in_=gt[hd][:, chunk(k)])
+                nc.vector.bn_stats(out=sts[NJ + hd][:, k, :], in_=gt[hd][:, chunk(k)])
 
-        def c_scalars(hd):
-            s = NJ + hd
-            nc.vector.bn_aggr(out=mv[:, s, :], in_=sts[hd][:].rearrange("p a s -> p (a s)"))
-            norm_scalars(s, v_bc[:, hd : hd + 1])
-
-        def c_next(hd, half):
+        def s_cn(hd, half):
             s = NJ + hd
             cs = chunk(half, W2)
-            eng("cn", hd).tensor_scalar(
-                out=gt[2 + hd][:, cs], in0=gt[hd][:, cs], scalar1=col(s, 9), scalar2=col(s, 11),
-                op0=ALU.mult, op1=ALU.add,
+            nc.vector.tensor_scalar(
+                out=gt[2 + hd][:, cs], in0=gt[hd][:, cs], scalar1=col(s, 9), scalar2=col(s, 11), op0=ALU.mult, op1=ALU.add
             )
 
-        def tanh_c(hd, half):
+        def s_th(hd, half):
             s = NJ + hd
             cs = chunk(half, W2)
-            nc.scalar.activation(
-                out=gt[6 + hd][:, cs], in_=gt[hd][:, cs], func=ACT.Tanh, scale=col(s, 9), bias=col(s, 11)
-            )
+            nc.scalar.activation(out=gt[6 + hd][:, cs], in_=gt[hd][:, cs], func=ACT.Tanh, scale=col(s, 9), bias=col(s, 11))
 
-        def mul_oh(hd, k, width):
+        def s_oh(hd, k, width):
             cs = chunk(k, width)
             nc.vector.tensor_tensor(out=gt[4 + hd][:, cs], in0=gt[4 + hd][:, cs], in1=gt[6 + hd][:, cs], op=ALU.mult)
 
-        x_product(0)
-        turn_bf16(wh, whT, 0, "hh")
-        turn_bf16(wh, whT, 1, "hh")
-        vec_turn(vra, pca, 8)
-        g2_consts()
-        turn_bf16(hr, hT, 0, "hh")
-        turn_bf16(hr, hT, 1, "hh")
-        x_product(1)
-        x_turn(0)
-        turn_bf16(hr, hT, 2, "hh")
-        turn_bf16(hr, hT, 3, "hh")
-        vec_turn(vrb, pcb, NV)
-        vec_consts()
-        hh_stage(0)
-        x_product(2)
-        x_turn(1)
-        w_turn(0)
-        w_turn(1)
-        x_product(3)
-        x_turn(2)
-        w_quant(0)
-        w_quant(1)
-        state["mx"] = True
-        x_quant(0)
-        x_quant(1)
-        x_turn(3)
-        x_quant(2)
-        x_quant(3)
-        ih_stats(ORDER[0])
-        for t in range(1, AHEAD):
-            hh_stage(t)
-            ih_stats(ORDER[t])
+        def f_out(tag, name, src, k):
+            t = psum.tile([P, 4, P], F32, tag=tag, bufs=BUFS[tag], name="pt")
+            ps[name] = t
+            for a in range(4):
+                nc.tensor.transpose(t[:, a, :], src[:, k * CW + a * P : k * CW + (a + 1) * P], identf[:])
 
-        def both(fn, hd):
-            fn(hd, 0)
-            fn(hd, 1)
+        def r_out(q_, name, k, hd, outv):
+            sg = work.tile([P, 4, P], F32, tag="sg", bufs=8, name="sg")
+            if q_ == "v":
+                nc.vector.tensor_copy(out=sg[:], in_=ps[name][:])
+            else:
+                nc.scalar.copy(out=sg[:], in_=ps[name][:])
+            nc.sync.dma_start(out=outv[:, 4 * k : 4 * k + 4, hd * P : (hd + 1) * P], in_=sg[:])
 
-        def fill_first(t):
-            if t == 0:
-                w_turn(3, "tp")
-                w_quant(3)
-                turn_bf16(cr, cT, 0, "tp")
-                turn_bf16(cr, cT, 1, "tp")
-            if t == 1:
-                turn_bf16(cr, cT, 2, "tp")
-                turn_bf16(cr, cT, 3, "tp")
-
-        def fill_last(t):
-            if t == 1:
-                mul_fc(0, 0)
-            if t == 2:
-                mul_fc(0, 1)
-                w_turn(2, "tp")
-                w_quant(2)
-            if t == 3:
-                both(mul_ig, 0)
-            if t == 4:
-                both(add_c, 0)
-                c_scalars(0)
-            if t == 5:
-                both(mul_fc, 1)
-                both(c_next, 0)
-                both(tanh_c, 0)
-                for k in range(NQ):
-                    store_turned(gt[2], k, 0, o0v, False)
-            if t == 6:
-                both(mul_ig, 1)
-                both(add_c, 1)
-                c_scalars(1)
-            if t == 7:
-                mul_oh(0, 0, W2)
-                mul_oh(0, 1, W2)
-                both(c_next, 1)
-                both(tanh_c, 1)
-                for k in range(NQ):
-                    store_turned(gt[4], k, 0, o1v, False)
-                    store_turned(gt[3], k, 1, o0v, False)
-
+        T_OF = {}
         for t in range(NJ):
-            j = ORDER[t]
-            fill_first(t)
-            fill_last(t)
+            T_OF[ORDER[t]] = t
+
+        def ok(t):
+            return 0 <= t < NJ
+
+        def pe_tb(what, src, q, tag):
+            fill(tag, (what, q), (), f_tb, src, q)
+
+        def rd_tb(q_, what, dst, q):
+            put(q_, ("r", what, q), ((what, q),), r_tb, q_, (what, q), dst, q)
+
+        def pe_vec(what, src):
+            fill("tp", (what,), (), f_vec, src)
+
+        def rd_vec(what, dst, n):
+            put("s", ("r", what), ((what,),), r_vec, (what,), dst, n)
+
+        def v_xp(q, parts):
+            for a in parts:
+                put("v", ("xp", q, a), (), s_xp, q, a)
+
+        def pe_x(q, half):
+            fill("ih", ("x", q, half), (("xp", q, 2 * half), ("xp", q, 2 * half + 1)), f_tw,
+                 lambda a: xbs[q][:, 2 * half + a, :])
+
+        def rd_x(q, half):
+            put("s", ("r", "x", q, half), (("x", q, half),), r_tw, ("x", q, half), lambda: x_dst(q, half))
+
+        def pe_w(pr, tag):
+            fill(tag, ("w", pr), (), f_tw, lambda a: wi[:, 2 * pr + a, :])
+
+        def rd_w(pr):
+            put("s", ("r", "w", pr), (("w", pr),), r_tw, ("w", pr), lambda: w_dst(pr))
+
+        def v_xq(q):
+            put("v", ("xq", q), (("r", "x", q, 0), ("r", "x", q, 1)), s_xq, q)
+
+        def v_wq(pr):
+            put("v", ("wq", pr), (("r", "w", pr),), s_wq, pr)
+
+        def pe_H(t, k):
+            if ok(t):
+                fill("hh", ("H", t, k), (("r", "wh", ORDER[t] // 4), ("r", "h", k)), f_hh, ORDER[t], k)
+
+        def rd_H(q_, t, k):
+            if ok(t):
+                put(q_, ("r", "H", t, k), (("H", t, k), ("r", "va")), r_hh, q_, ("H", t, k), ORDER[t], k)
+
+        def g_G1(t):
+            if ok(t):
+                put("g", ("G1", t), [("r", "H", t, k) for k in range(NQ)], s_g1, ORDER[t])
+
+        def s_Q(t):
+            if ok(t):
+                put("s", ("Q", t), (("G1", t),), s_q, ORDER[t])
+
+        def g_G2(t):
+            if ok(t):
+                put("g", ("G2", t), (("Q", t), ("g2c",), ("vc",)), s_g2, ORDER[t])
+
+        def g_G23(ta, tb):
+            needs = [("g2c",), ("vc",)]
+            if ok(ta):
+                needs += [("NA", ta), ("G2", ta)]
+            if ok(tb):
+                needs += [("Q", tb)]
+            if ok(ta) or ok(tb):
+                put("g", ("G23", ta, tb), needs, s_g23, ORDER[ta] if ok(ta) else None, ORDER[tb] if ok(tb) else None)
+
+        def pe_M(stage, t, k):
+            if ok(t):
+                fill("ih", (stage, t, k), (("wq", ORDER[t] // 2), ("xq", k)), f_mx, ORDER[t], k)
+
+        def v_N(t, k):
+            if ok(t):
+                put("v", ("r", "N", t, k), (("N", t, k),), r_bn, ("N", t, k), ORDER[t], k)
+
+        def v_NA(t):
+            if ok(t):
+                put("v", ("NA", t), [("r", "N", t, k) for k in range(NQ)], s_aggr, ORDER[t], ORDER[t])
+
+        def g_G3(t):
+            if ok(t):
+                put("g", ("G3", t), (("NA", t), ("G2", t)), s_norm, ORDER[t], col(ORDER[t], 12))
+
+        def v_J(t, k):
+            if ok(t):
+                put("v", ("r", "J", t, k), (("J", t, k), ("G3", t), ("Q", t), ("r", "H", t, k)), r_join,
+                    ("J", t, k), ORDER[t], k)
+
+        def s_A(t, half):
+            if ok(t):
+                put("s", ("A", t, half), (("r", "J", t, 2 * half), ("r", "J", t, 2 * half + 1)), s_act, ORDER[t], half)
+
+        def x_fc(q_, hd, half):
+            put(q_, ("fc", hd, half), (("A", T_OF[hd], half), ("r", "c", 2 * half), ("r", "c", 2 * half + 1)),
+                s_fc, q_, hd, half)
+
+        def x_ig(q_, hd, half):
+            put(q_, ("ig", hd, half), (("A", T_OF[2 + hd], half), ("A", T_OF[6 + hd], half)), s_ig, q_, hd, half)
+
+        def v_add(hd, half):
+            put("v", ("add", hd, half), (("fc", hd, half), ("ig", hd, half)), s_add, hd, half)
+
+        def v_ca(hd):
+            put("v", ("ca", hd), (("add", hd, 0), ("add", hd, 1)), s_aggr, NJ + hd, NJ + hd)
+
+        def g_cs(hd):
+            put("g", ("cs", hd), (("ca", hd), ("vc",)), s_norm, NJ + hd, v_bc[:, hd : hd + 1])
+
+        def v_cn(hd, half):
+            put("v", ("cn", hd, half), (("cs", hd),), s_cn, hd, half)
+
+        def s_TH(hd, half):
+            put("s", ("th", hd, half), (("cs", hd),), s_th, hd, half)
+
+        def v_oh(hd, k, width):
+            half = k * width // W2
+            put("v", ("oh", hd, k), (("A", T_OF[4 + hd], half), ("th", hd, half)), s_oh, hd, k, width)
+
+        def pe_oc(hd, k, tag):
+            fill(tag, ("oc", hd, k), (("cn", hd, k // 2),), f_out, gt[2 + hd], k)
+
+        def rd_oc(q_, hd, k):
+            put(q_, ("r", "oc", hd, k), (("oc", hd, k),), r_out, q_, ("oc", hd, k), k, hd, o0v)
+
+        def pe_ho(hd, k, tag, width):
+            fill(tag, ("ho", hd, k), (("oh", hd, k * CW // width),), f_out, gt[4 + hd], k)
+
+        def rd_ho(q_, hd, k):
+            put(q_, ("r", "ho", hd, k), (("ho", hd, k),), r_out, q_, ("ho", hd, k), k, hd, o1v)
+
+        def run():
+            done = set()
+            pos = {"pe": 0, "v": 0, "s": 0, "g": 0}
+            left = sum(len(queues[q]) for q in pos)
+            while left > 0:
+                moved = 0
+                for q in ("pe", "v", "s", "g"):
+                    lst = queues[q]
+                    while pos[q] < len(lst) and all(n in done for n in lst[pos[q]][1]):
+                        name, needs, fn, args = lst[pos[q]]
+                        fn(*args)
+                        done.add(name)
+                        if name[0] == "G23":
+                            done.add(("G3", name[1]))
+                            done.add(("G2", name[2]))
+                        pos[q] += 1
+                        moved += 1
+                assert moved > 0, [queues[q][pos[q]][0:2] for q in pos if pos[q] < len(queues[q])]
+                left -= moved
+
+        LH = 3
+        LN = 2
+
+        v_xp(0, (0, 1, 2, 3))
+        v_xp(1, (0, 1, 2, 3))
+        v_xp(2, (0,))
+        rd_H("v", 0, 0)
+        v_xp(2, (1, 2, 3))
+        v_xp(3, (0,))
+        rd_H("v", 0, 1)
+        v_xp(3, (1, 2, 3))
+        v_wq(0)
+        v_wq(1)
+        v_xq(0)
+        v_xq(1)
+        rd_H("v", 1, 0)
+        v_xq(2)
+        rd_H("v", 1, 1)
+        v_N(0, 0)
+        v_N(0, 1)
+        rd_H("v", 2, 0)
+        v_N(0, 2)
+        v_xq(3)
+        v_N(1, 0)
+        v_N(1, 1)
+        v_N(1, 2)
+        v_N(0, 3)
+        v_wq(3)
+        v_NA(0)
+        v_N(1, 3)
+        rd_H("v", 2, 1)
+        v_NA(1)
+        rd_H("v", 3, 0)
+        rd_H("v", 3, 1)
+        for t in range(NJ):
             for k in range(NQ):
-                combine(j, k)
-                if k % 2 == 1:
-                    activate(j, k // 2)
-            if t + AHEAD < NJ:
-                hh_stage(t + AHEAD)
-                ih_stats(ORDER[t + AHEAD])
+                v_J(t, k)
+                if t == 5 and k == 0:
+                    v_ca(0)
+            if t == 2:
+                v_wq(2)
+            if t == 6:
+                v_cn(0, 0)
+                v_cn(0, 1)
+            if t == 7:
+                v_add(1, 0)
+                v_add(1, 1)
+                v_oh(0, 0, W2)
+                v_ca(1)
+                v_oh(0, 1, W2)
+                v_cn(1, 0)
+                v_cn(1, 1)
+            for k in range(NQ):
+                v_N(t + LN, k)
+            rd_H("v", t + LH + 1, 0)
+            v_NA(t + LN)
+            rd_H("v", t + LH + 1, 1)
+            if t == 3:
+                v_add(0, 0)
+            if t == 4:
+                v_add(0, 1)
+        rd_ho("v", 0, 0)
+        v_oh(1, 0, CW)
+        v_oh(1, 1, CW)
+        rd_ho("v", 0, 1)
+        v_oh(1, 2, CW)
+        v_oh(1, 3, CW)
+        rd_ho("v", 0, 2)
+        rd_ho("v", 0, 3)
+
+        rd_tb("s", "wh", whT, 0)
+        rd_tb("s", "wh", whT, 1)
+        rd_tb("s", "h", hT, 0)
+        rd_tb("s", "h", hT, 1)
+        rd_x(0, 0)
+        rd_x(0, 1)
+        rd_vec("va", pca, 8)
+        rd_w(0)
+        rd_tb("s", "h", hT, 2)
+        rd_vec("vb", pcb, NV)
+        rd_x(1, 0)
+        rd_tb("s", "h", hT, 3)
+        rd_x(1, 1)
+        rd_w(1)
+        rd_x(2, 0)
+        rd_H("s", 0, 2)
+        rd_H("s", 0, 3)
+        rd_x(2, 1)
+        rd_x(3, 0)
+        s_Q(0)
+        rd_x(3, 1)
+        rd_H("s", 1, 2)
+        rd_H("s", 1, 3)
+        rd_w(3)
+        rd_tb("s", "c", cT, 0)
+        s_Q(1)
+        rd_H("s", 2, 2)
+        rd_H("s", 2, 3)
+        rd_tb("s", "c", cT, 1)
+        s_Q(2)
+        for t in range(NJ):
+            rd_H("s", t + LH, 2)
+            rd_H("s", t + LH, 3)
+            s_A(t, 0)
+            s_A(t, 1)
+            if t == 0:
+                rd_tb("s", "c", cT, 2)
+            if t == 1:
+                rd_tb("s", "c", cT, 3)
+                rd_w(2)
+            s_Q(t + LH)
+            if t == 5:
+                s_TH(0, 0)
+                s_TH(0, 1)
+            if t == 6:
+                for k in range(NQ):
+                    rd_oc("s", 0, k)
+            if t == 7:
+                s_TH(1, 0)
+                s_TH(1, 1)
         for k in range(NQ):
-            mul_oh(1, k, CW)
-            store_turned(gt[5], k, 1, o1v, k >= 2, "ih")
+            rd_oc("s", 1, k)
+        for k in range(NQ):
+            rd_ho("s", 1, k)
+
+        put("g", ("g2c",), (("r", "va"),), s_g2c)
+        put("g", ("vc",), (("r", "vb"),), s_vc)
+        g_G1(0)
+        g_G23(-1, 0)
+        g_G1(1)
+        g_G23(-1, 1)
+        g_G1(2)
+        g_G23(0, -1)
+        for t in range(NJ):
+            g_G23(t + 1, t + 2)
+            g_G1(t + LH)
+            if t < 2:
+                x_fc("g", 0, t)
+            if t == 2:
+                x_ig("g", 0, 0)
+            if t == 3:
+                x_ig("g", 0, 1)
+            if t == 4:
+                x_fc("g", 1, 0)
+                x_fc("g", 1, 1)
+            if t == 5:
+                g_cs(0)
+            if t == 6:
+                x_ig("g", 1, 0)
+                x_ig("g", 1, 1)
+            if t == 7:
+                g_cs(1)
+
+        pe_tb("wh", wh, 0, "hh")
+        pe_tb("wh", wh, 1, "hh")
+        pe_tb("h", hr, 0, "hh")
+        pe_tb("h", hr, 1, "hh")
+        pe_x(0, 0)
+        pe_w(0, "ih")
+        pe_x(0, 1)
+        pe_vec("va", vra)
+        pe_H(0, 0)
+        pe_tb("h", hr, 2, "hh")
+        pe_x(1, 0)
+        pe_x(1, 1)
+        pe_vec("vb", vrb)
+        pe_w(1, "ih")
+        pe_tb("h", hr, 3, "hh")
+        pe_H(0, 1)
+        pe_x(2, 0)
+        pe_w(3, "tp")
+        pe_tb("c", cr, 0, "tp")
+        pe_H(0, 2)
+        pe_H(0, 3)
+        pe_x(2, 1)
+        pe_x(3, 0)
+        pe_H(1, 0)
+        pe_H(1, 1)
+        pe_x(3, 1)
+        pe_H(1, 2)
+        pe_M("N", 0, 0)
+        pe_H(1, 3)
+        pe_M("N", 0, 1)
+        pe_H(2, 0)
+        pe_M("N", 0, 2)
+        pe_M("N", 1, 0)
+        pe_M("N", 1, 1)
+        pe_H(2, 2)
+        pe_M("N", 1, 2)
+        pe_H(2, 3)
+        pe_M("N", 0, 3)
+        pe_tb("c", cr, 1, "tp")
+        pe_M("N", 1, 3)
+        pe_H(2, 1)
+        pe_H(3, 0)
+        pe_H(3, 1)
+        for t in range(NJ):
+            pe_H(t + LH, 2)
+            pe_M("J", t, 0)
+            pe_H(t + LH, 3)
+            pe_M("J", t, 1)
+            pe_M("J", t, 2)
+            pe_M("J", t, 3)
+            if t == 7:
+                for k in range(NQ):
+                    pe_oc(0, k, "tp")
+            if t == 0:
+                pe_tb("c", cr, 2, "tp")
+            if t == 1:
+                pe_tb("c", cr, 3, "tp")
+                pe_w(2, "tp")
+            pe_M("N", t + LN, 0)
+            pe_M("N", t + LN, 1)
+            pe_H(t + LH + 1, 0)
+            pe_M("N", t + LN, 2)
+            pe_H(t + LH + 1, 1)
+            pe_M("N", t + LN, 3)
+        for k in range(NQ):
+            pe_ho(0, k, "hh", W2)
+            pe_oc(1, k, "tp")
+        for k in range(NQ):
+            pe_ho(1, k, "ih", CW)
+        run()

@@ -22,7 +22,7 @@ NQ = 4
 CW = 512
 NJ = 8
 ORDER = (0, 2, 6, 1, 3, 7, 4, 5)
-V_SHARE = (2, 2, 2, 2, 2, 2, 1, 1)
+V_SHARE = (2, 2, 2, 2, 2, 2, 2, 2)
 ON_GPSIMD = ("fc0", "ig0", "fc1")
 WARM = 6
 PLAIN_DUMMIES = 10
@@ -129,12 +129,13 @@ def tile_lstmcell_kernel(
         o0v = out_0.rearrange("(p n) c -> p n c", n=NB)
         o1v = out_1.rearrange("(p n) c -> p n c", n=NB)
         W2 = 2 * CW
-        ps, xbs, xgs, wgs, sts = {}, {}, {}, {}, {}
+        ps, xbs, xgs, wgs, sts, sgs = {}, {}, {}, {}, {}, {}
+        SG_BUFS = 16
 
         def col(j, i):
             return gw[:, j, i : i + 1]
 
-        queues = {"pe": [], "v": [], "s": [], "g": []}
+        queues = {"pe": [], "v": [], "s": [], "g": [], "sp": []}
         rings = {"ih": [], "hh": [], "tp": []}
         BUFS = {"ih": IH_BUFS, "hh": HH_BUFS, "tp": TP_BUFS}
 
@@ -384,13 +385,16 @@ def tile_lstmcell_kernel(
             for a in range(4):
                 nc.tensor.transpose(t[:, a, :], src[:, k * CW + a * P : k * CW + (a + 1) * P], identf[:])
 
-        def r_out(q_, name, k, hd, outv):
-            sg = work.tile([P, 4, P], F32, tag="sg", bufs=8, name="sg")
+        def r_out(q_, name):
+            sg = work.tile([P, 4, P], F32, tag="sg", bufs=SG_BUFS, name="sg")
+            sgs[name] = sg
             if q_ == "v":
                 nc.vector.tensor_copy(out=sg[:], in_=ps[name][:])
             else:
                 nc.scalar.copy(out=sg[:], in_=ps[name][:])
-            nc.sync.dma_start(out=outv[:, 4 * k : 4 * k + 4, hd * P : (hd + 1) * P], in_=sg[:])
+
+        def s_store(name, k, hd, outv):
+            nc.sync.dma_start(out=outv[:, 4 * k : 4 * k + 4, hd * P : (hd + 1) * P], in_=sgs[name][:])
 
         T_OF = {}
         for t in range(NJ):
@@ -518,21 +522,27 @@ def tile_lstmcell_kernel(
             fill(tag, ("oc", hd, k), (("cn", hd, k // 2),), f_out, gt[2 + hd], k)
 
         def rd_oc(q_, hd, k):
-            put(q_, ("r", "oc", hd, k), (("oc", hd, k),), r_out, q_, ("oc", hd, k), k, hd, o0v)
+            put(q_, ("r", "oc", hd, k), (("oc", hd, k),), r_out, q_, ("oc", hd, k))
+
+        def st_oc(hd, k):
+            put("sp", ("st", "oc", hd, k), (("r", "oc", hd, k),), s_store, ("oc", hd, k), k, hd, o0v)
 
         def pe_ho(hd, k, tag, width):
             fill(tag, ("ho", hd, k), (("oh", hd, k * CW // width),), f_out, gt[4 + hd], k)
 
         def rd_ho(q_, hd, k):
-            put(q_, ("r", "ho", hd, k), (("ho", hd, k),), r_out, q_, ("ho", hd, k), k, hd, o1v)
+            put(q_, ("r", "ho", hd, k), (("ho", hd, k),), r_out, q_, ("ho", hd, k))
+
+        def st_ho(hd, k):
+            put("sp", ("st", "ho", hd, k), (("r", "ho", hd, k),), s_store, ("ho", hd, k), k, hd, o1v)
 
         def run():
             done = set()
-            pos = {"pe": 0, "v": 0, "s": 0, "g": 0}
+            pos = {"pe": 0, "v": 0, "s": 0, "g": 0, "sp": 0}
             left = sum(len(queues[q]) for q in pos)
             while left > 0:
                 moved = 0
-                for q in ("pe", "v", "s", "g"):
+                for q in ("pe", "v", "s", "g", "sp"):
                     lst = queues[q]
                     while pos[q] < len(lst) and all(n in done for n in lst[pos[q]][1]):
                         name, needs, fn, args = lst[pos[q]]
@@ -548,6 +558,9 @@ def tile_lstmcell_kernel(
 
         LH = 3
         LN = 2
+
+        def share(t):
+            return V_SHARE[t] if ok(t) else 2
 
         v_xp(0, (0, 1, 2, 3))
         v_xp(1, (0, 1, 2, 3))
@@ -593,8 +606,8 @@ def tile_lstmcell_kernel(
             if t == 7:
                 v_add(1, 0)
                 v_add(1, 1)
-                v_oh(0, 0, W2)
                 v_ca(1)
+                v_oh(0, 0, W2)
                 v_oh(0, 1, W2)
                 v_cn(1, 0)
                 v_cn(1, 1)
@@ -602,7 +615,8 @@ def tile_lstmcell_kernel(
                 v_N(t + LN, k)
             rd_H("v", t + LH + 1, 0)
             v_NA(t + LN)
-            rd_H("v", t + LH + 1, 1)
+            if share(t + LH + 1) > 1:
+                rd_H("v", t + LH + 1, 1)
             if t == 3:
                 v_add(0, 0)
             if t == 4:
@@ -615,6 +629,8 @@ def tile_lstmcell_kernel(
         v_oh(1, 3, CW)
         rd_ho("v", 0, 2)
         rd_ho("v", 0, 3)
+        rd_ho("v", 1, 2)
+        rd_ho("v", 1, 3)
 
         rd_tb("s", "wh", whT, 0)
         rd_tb("s", "wh", whT, 1)
@@ -647,8 +663,8 @@ def tile_lstmcell_kernel(
         rd_tb("s", "c", cT, 1)
         s_Q(2)
         for t in range(NJ):
-            rd_H("s", t + LH, 2)
-            rd_H("s", t + LH, 3)
+            for k in range(share(t + LH), NQ):
+                rd_H("s", t + LH, k)
             s_A(t, 0)
             s_A(t, 1)
             if t == 0:
@@ -668,17 +684,17 @@ def tile_lstmcell_kernel(
                 s_TH(1, 1)
         for k in range(NQ):
             rd_oc("s", 1, k)
-        for k in range(NQ):
-            rd_ho("s", 1, k)
+        rd_ho("s", 1, 0)
+        rd_ho("s", 1, 1)
 
         put("g", ("g2c",), (("r", "va"),), s_g2c)
         put("g", ("vc",), (("r", "vb"),), s_vc)
         g_G1(0)
         g_G23(-1, 0)
         g_G1(1)
-        g_G23(-1, 1)
-        g_G1(2)
         g_G23(0, -1)
+        g_G1(2)
+        g_G23(-1, 1)
         for t in range(NJ):
             g_G23(t + 1, t + 2)
             g_G1(t + LH)
@@ -743,6 +759,8 @@ def tile_lstmcell_kernel(
         pe_H(3, 0)
         pe_H(3, 1)
         for t in range(NJ):
+            if share(t + LH) < 2:
+                pe_H(t + LH, 1)
             pe_H(t + LH, 2)
             pe_M("J", t, 0)
             pe_H(t + LH, 3)
@@ -759,13 +777,22 @@ def tile_lstmcell_kernel(
                 pe_w(2, "tp")
             pe_M("N", t + LN, 0)
             pe_M("N", t + LN, 1)
-            pe_H(t + LH + 1, 0)
             pe_M("N", t + LN, 2)
-            pe_H(t + LH + 1, 1)
             pe_M("N", t + LN, 3)
+            pe_H(t + LH + 1, 0)
+            if share(t + LH + 1) > 1:
+                pe_H(t + LH + 1, 1)
         for k in range(NQ):
             pe_ho(0, k, "hh", W2)
             pe_oc(1, k, "tp")
         for k in range(NQ):
             pe_ho(1, k, "ih", CW)
+
+        for k in range(NQ):
+            st_oc(0, k)
+        for k in range(NQ):
+            st_ho(0, k)
+            st_oc(1, k)
+        for k in range(NQ):
+            st_ho(1, k)
         run()

@@ -129,7 +129,7 @@ def tile_lstmcell_kernel(
         o0v = out_0.rearrange("(p n) c -> p n c", n=NB)
         o1v = out_1.rearrange("(p n) c -> p n c", n=NB)
         W2 = 2 * CW
-        ps, xbs, xgs, wgs, sts, sgs = {}, {}, {}, {}, {}, {}
+        ps, xbs, xgs, wgs, sts, sgs, ths = {}, {}, {}, {}, {}, {}, {}
         SG_BUFS = 16
 
         def col(j, i):
@@ -146,8 +146,8 @@ def tile_lstmcell_kernel(
             ring = rings[tag]
             needs = tuple(needs)
             if len(ring) >= BUFS[tag]:
-                needs = needs + (ring[len(ring) - BUFS[tag]],)
-            ring.append(("r",) + name)
+                needs = needs + ring[len(ring) - BUFS[tag]]
+            ring.append((("r",) + name, ("tT",) + name[1:]) if name[0] == "oc" else (("r",) + name,))
             put("pe", name, needs, fn, tag, name, *args)
 
         def engine(q):
@@ -370,14 +370,15 @@ def tile_lstmcell_kernel(
                 out=gt[2 + hd][:, cs], in0=gt[hd][:, cs], scalar1=col(s, 9), scalar2=col(s, 11), op0=ALU.mult, op1=ALU.add
             )
 
-        def s_th(hd, half):
-            s = NJ + hd
-            cs = chunk(half, W2)
-            nc.scalar.activation(out=gt[6 + hd][:, cs], in_=gt[hd][:, cs], func=ACT.Tanh, scale=col(s, 9), bias=col(s, 11))
+        def s_tanh(name):
+            th = work.tile([P, 4, P], F32, tag="th", bufs=8, name="th")
+            ths[name] = th
+            nc.scalar.activation(out=th[:], in_=ps[name][:], func=ACT.Tanh)
 
-        def s_oh(hd, k, width):
-            cs = chunk(k, width)
-            nc.vector.tensor_tensor(out=gt[4 + hd][:, cs], in0=gt[4 + hd][:, cs], in1=gt[6 + hd][:, cs], op=ALU.mult)
+        def r_prod(name, cname):
+            sg = work.tile([P, 4, P], F32, tag="sg", bufs=SG_BUFS, name="sg")
+            sgs[name] = sg
+            nc.vector.tensor_tensor(out=sg[:], in0=ps[name][:], in1=ths[cname][:], op=ALU.mult)
 
         def f_out(tag, name, src, k):
             t = psum.tile([P, 4, P], F32, tag=tag, bufs=BUFS[tag], name="pt")
@@ -511,12 +512,8 @@ def tile_lstmcell_kernel(
         def v_cn(hd, half):
             put("v", ("cn", hd, half), (("cs", hd),), s_cn, hd, half)
 
-        def s_TH(hd, half):
-            put("s", ("th", hd, half), (("cs", hd),), s_th, hd, half)
-
-        def v_oh(hd, k, width):
-            half = k * width // W2
-            put("v", ("oh", hd, k), (("A", T_OF[4 + hd], half), ("th", hd, half)), s_oh, hd, k, width)
+        def s_tT(hd, k):
+            put("s", ("tT", hd, k), (("oc", hd, k),), s_tanh, ("oc", hd, k))
 
         def pe_oc(hd, k, tag):
             fill(tag, ("oc", hd, k), (("cn", hd, k // 2),), f_out, gt[2 + hd], k)
@@ -527,11 +524,11 @@ def tile_lstmcell_kernel(
         def st_oc(hd, k):
             put("sp", ("st", "oc", hd, k), (("r", "oc", hd, k),), s_store, ("oc", hd, k), k, hd, o0v)
 
-        def pe_ho(hd, k, tag, width):
-            fill(tag, ("ho", hd, k), (("oh", hd, k * CW // width),), f_out, gt[4 + hd], k)
+        def pe_ho(hd, k, tag):
+            fill(tag, ("ho", hd, k), (("A", T_OF[4 + hd], k // 2),), f_out, gt[4 + hd], k)
 
-        def rd_ho(q_, hd, k):
-            put(q_, ("r", "ho", hd, k), (("ho", hd, k),), r_out, q_, ("ho", hd, k))
+        def rd_ho(hd, k):
+            put("v", ("r", "ho", hd, k), (("ho", hd, k), ("tT", hd, k)), r_prod, ("ho", hd, k), ("oc", hd, k))
 
         def st_ho(hd, k):
             put("sp", ("st", "ho", hd, k), (("r", "ho", hd, k),), s_store, ("ho", hd, k), k, hd, o1v)
@@ -607,8 +604,8 @@ def tile_lstmcell_kernel(
                 v_add(1, 0)
                 v_add(1, 1)
                 v_ca(1)
-                v_oh(0, 0, W2)
-                v_oh(0, 1, W2)
+                for k in range(NQ):
+                    rd_ho(0, k)
                 v_cn(1, 0)
                 v_cn(1, 1)
             for k in range(NQ):
@@ -621,16 +618,9 @@ def tile_lstmcell_kernel(
                 v_add(0, 0)
             if t == 4:
                 v_add(0, 1)
-        rd_ho("v", 0, 0)
-        v_oh(1, 0, CW)
-        v_oh(1, 1, CW)
-        rd_ho("v", 0, 1)
-        v_oh(1, 2, CW)
-        v_oh(1, 3, CW)
-        rd_ho("v", 0, 2)
-        rd_ho("v", 0, 3)
-        rd_ho("v", 1, 2)
-        rd_ho("v", 1, 3)
+        for k in range(NQ):
+            rd_oc("v", 1, k)
+            rd_ho(1, k)
 
         rd_tb("s", "wh", whT, 0)
         rd_tb("s", "wh", whT, 1)
@@ -673,19 +663,12 @@ def tile_lstmcell_kernel(
                 rd_tb("s", "c", cT, 3)
                 rd_w(2)
             s_Q(t + LH)
-            if t == 5:
-                s_TH(0, 0)
-                s_TH(0, 1)
             if t == 6:
                 for k in range(NQ):
+                    s_tT(0, k)
                     rd_oc("s", 0, k)
-            if t == 7:
-                s_TH(1, 0)
-                s_TH(1, 1)
         for k in range(NQ):
-            rd_oc("s", 1, k)
-        rd_ho("s", 1, 0)
-        rd_ho("s", 1, 1)
+            s_tT(1, k)
 
         put("g", ("g2c",), (("r", "va"),), s_g2c)
         put("g", ("vc",), (("r", "vb"),), s_vc)
@@ -783,16 +766,16 @@ def tile_lstmcell_kernel(
             if share(t + LH + 1) > 1:
                 pe_H(t + LH + 1, 1)
         for k in range(NQ):
-            pe_ho(0, k, "hh", W2)
-            pe_oc(1, k, "tp")
+            pe_ho(0, k, "hh")
         for k in range(NQ):
-            pe_ho(1, k, "ih", CW)
+            pe_oc(1, k, "tp")
+            pe_ho(1, k, "ih")
 
         for k in range(NQ):
             st_oc(0, k)
         for k in range(NQ):
             st_ho(0, k)
-            st_oc(1, k)
         for k in range(NQ):
+            st_oc(1, k)
             st_ho(1, k)
         run()

@@ -354,21 +354,29 @@ def tile_lstmcell_kernel(
             cs = chunk(half, W2)
             engine(q_).tensor_tensor(out=gt[2 + hd][:, cs], in0=gt[2 + hd][:, cs], in1=gt[6 + hd][:, cs], op=ALU.mult)
 
-        def s_add(hd, half):
+        def s_add(q_, hd, half):
             cs = chunk(half, W2)
+            engine(q_).tensor_tensor(out=gt[hd][:, cs], in0=gt[hd][:, cs], in1=gt[2 + hd][:, cs], op=ALU.add)
+
+        def s_bnc(hd, half):
             if half == 0:
                 st3 = work.tile([P, NQ, 6], F32, tag="st", bufs=4, name="st3")
                 sts[NJ + hd] = st3
-            nc.vector.tensor_tensor(out=gt[hd][:, cs], in0=gt[hd][:, cs], in1=gt[2 + hd][:, cs], op=ALU.add)
             for k in (2 * half, 2 * half + 1):
                 nc.vector.bn_stats(out=sts[NJ + hd][:, k, :], in_=gt[hd][:, chunk(k)])
 
-        def s_cn(hd, half):
+        def s_cn(q_, hd, half):
             s = NJ + hd
             cs = chunk(half, W2)
-            nc.vector.tensor_scalar(
-                out=gt[2 + hd][:, cs], in0=gt[hd][:, cs], scalar1=col(s, 9), scalar2=col(s, 11), op0=ALU.mult, op1=ALU.add
-            )
+            if q_ == "s":
+                nc.scalar.activation(
+                    out=gt[2 + hd][:, cs], in_=gt[hd][:, cs], func=ACT.Identity, scale=col(s, 9), bias=col(s, 11)
+                )
+            else:
+                engine(q_).tensor_scalar(
+                    out=gt[2 + hd][:, cs], in0=gt[hd][:, cs], scalar1=col(s, 9), scalar2=col(s, 11),
+                    op0=ALU.mult, op1=ALU.add,
+                )
 
         def s_tanh(name):
             th = work.tile([P, 4, P], F32, tag="th", bufs=8, name="th")
@@ -500,17 +508,27 @@ def tile_lstmcell_kernel(
         def x_ig(q_, hd, half):
             put(q_, ("ig", hd, half), (("A", T_OF[2 + hd], half), ("A", T_OF[6 + hd], half)), s_ig, q_, hd, half)
 
+        def x_add(q_, hd, half):
+            put(q_, ("add", hd, half), (("fc", hd, half), ("ig", hd, half)), s_add, q_, hd, half)
+
+        def v_bnc(hd, half):
+            put("v", ("bnc", hd, half), (("add", hd, half),), s_bnc, hd, half)
+
         def v_add(hd, half):
-            put("v", ("add", hd, half), (("fc", hd, half), ("ig", hd, half)), s_add, hd, half)
+            x_add("v", hd, half)
+            v_bnc(hd, half)
 
         def v_ca(hd):
-            put("v", ("ca", hd), (("add", hd, 0), ("add", hd, 1)), s_aggr, NJ + hd, NJ + hd)
+            put("v", ("ca", hd), (("bnc", hd, 0), ("bnc", hd, 1)), s_aggr, NJ + hd, NJ + hd)
 
         def g_cs(hd):
             put("g", ("cs", hd), (("ca", hd), ("vc",)), s_norm, NJ + hd, v_bc[:, hd : hd + 1])
 
+        def x_cn(q_, hd, half):
+            put(q_, ("cn", hd, half), (("cs", hd),), s_cn, q_, hd, half)
+
         def v_cn(hd, half):
-            put("v", ("cn", hd, half), (("cs", hd),), s_cn, hd, half)
+            x_cn("v", hd, half)
 
         def s_tT(hd, k):
             put("s", ("tT", hd, k), (("oc", hd, k),), s_tanh, ("oc", hd, k))
@@ -519,7 +537,7 @@ def tile_lstmcell_kernel(
             fill(tag, ("oc", hd, k), (("cn", hd, k // 2),), f_out, gt[2 + hd], k)
 
         def rd_oc(q_, hd, k):
-            put(q_, ("r", "oc", hd, k), (("oc", hd, k),), r_out, q_, ("oc", hd, k))
+            put(q_, ("r", "oc", hd, k), (("oc", hd, k), ("tT", hd, k)), r_out, q_, ("oc", hd, k))
 
         def st_oc(hd, k):
             put("sp", ("st", "oc", hd, k), (("r", "oc", hd, k),), s_store, ("oc", hd, k), k, hd, o0v)
@@ -670,9 +688,9 @@ def tile_lstmcell_kernel(
         for k in range(NQ):
             s_tT(1, k)
 
+        g_G1(0)
         put("g", ("g2c",), (("r", "va"),), s_g2c)
         put("g", ("vc",), (("r", "vb"),), s_vc)
-        g_G1(0)
         g_G23(-1, 0)
         g_G1(1)
         g_G23(0, -1)

@@ -688,9 +688,9 @@ def tile_lstmcell_kernel(
         for k in range(NQ):
             s_tT(1, k)
 
-        g_G1(0)
         put("g", ("g2c",), (("r", "va"),), s_g2c)
         put("g", ("vc",), (("r", "vb"),), s_vc)
+        g_G1(0)
         g_G23(-1, 0)
         g_G1(1)
         g_G23(0, -1)

@@ -251,6 +251,49 @@ def tile_lstmcell_kernel(
                     accum_out=sy[:, j, k : k + 1],
                 )
 
+        sw = keep.tile([P, NJ + 2, 16], F32, name="sw")
+        rr = keep.tile([P, NJ + 2, 2], F32, name="rr")
+        epst = keep.tile([P, 1], F32, name="epst")
+        nc.gpsimd.memset(epst[:], EPS)
+
+        def sc_(slot, i):
+            return sw[:, slot, i : i + 1]
+
+        def fma(out, in_, scale, bias=None):
+            if bias is None:
+                nc.scalar.activation(out=out, in_=in_, func=ACT.Identity, scale=scale)
+            else:
+                nc.scalar.activation(out=out, in_=in_, func=ACT.Identity, scale=scale, bias=bias)
+
+        def s_s1(j):
+            nc.scalar.activation(
+                out=sw[:, j, 9:13], in_=sy[:, j, :], func=ACT.Identity, scale=-1.0 / B, accum_out=sc_(j, 2)
+            )
+
+        def s_s2(j):
+            fma(sc_(j, 1), qy[:, j : j + 1], igb[:, j : j + 1], epst[:])
+
+        def s_s5(slot):
+            fma(sc_(slot, 0), mv[:, slot, 1:2], 1.0, epst[:])
+
+        def s_pow(slot, n):
+            nc.gpsimd.tensor_tensor(out=rr[:, slot, 0:n], in0=sw[:, slot, 0:n], in1=expo[:, 8 : 8 + n], op=ALU.pow)
+
+        def s_s6(j):
+            r1, r2 = rr[:, j, 0:1], rr[:, j, 1:2]
+            fma(sc_(j, 3), sc_(j, 1), r2)
+            fma(sc_(j, 5), r1, v_g1[:, j : j + 1])
+            fma(sc_(j, 6), r1, col(j, 7))
+            fma(sc_(j, 4), sc_(j, 2), r2, bsum[:, j : j + 1])
+            fma(sc_(j, 7), sc_(j, 3), sc_(j, 5))
+            fma(sc_(j, 8), mv[:, j, 0:1], sc_(j, 6), sc_(j, 4))
+
+        def s_s7(hd):
+            s = NJ + hd
+            fma(sc_(s, 7), rr[:, s, 0:1], v_gc[:, hd : hd + 1])
+            fma(sc_(s, 6), rr[:, s, 0:1], col(s, 7))
+            fma(sc_(s, 8), mv[:, s, 0:1], sc_(s, 6), v_bc[:, hd : hd + 1])
+
         def s_g1(j):
             nc.gpsimd.tensor_tensor(out=gw[:, j, 0:2], in0=sy[:, j, 0:2], in1=sy[:, j, 2:4], op=ALU.add)
             nc.gpsimd.tensor_scalar(
@@ -259,7 +302,7 @@ def tile_lstmcell_kernel(
 
         def s_q(j):
             junk = work.tile([P, B], BF16, tag="junk", name="junk")
-            nc.scalar.activation(out=junk[:], in_=gt[j][:], func=ACT.Square, bias=col(j, 2), accum_out=qy[:, j : j + 1])
+            nc.scalar.activation(out=junk[:], in_=gt[j][:], func=ACT.Square, bias=sc_(j, 2), accum_out=qy[:, j : j + 1])
 
         def s_g2(j):
             nc.gpsimd.tensor_scalar(
@@ -336,14 +379,14 @@ def tile_lstmcell_kernel(
 
         def r_join(name, j, k):
             nc.vector.scalar_tensor_tensor(
-                out=gt[j][:, chunk(k)], in0=ps[name][:], scalar=col(j, 9), in1=gt[j][:, chunk(k)],
+                out=gt[j][:, chunk(k)], in0=ps[name][:], scalar=sc_(j, 7), in1=gt[j][:, chunk(k)],
                 op0=ALU.mult, op1=ALU.add,
             )
 
         def s_act(j, half):
             nc.scalar.activation(
                 out=gt[j][:, chunk(half, W2)], in_=gt[j][:, chunk(half, W2)],
-                func=(ACT.Tanh if j >= 6 else ACT.Sigmoid), scale=col(j, 4), bias=col(j, 11),
+                func=(ACT.Tanh if j >= 6 else ACT.Sigmoid), scale=rr[:, j, 1:2], bias=sc_(j, 8),
             )
 
         def s_fc(q_, hd, half):
@@ -370,11 +413,11 @@ def tile_lstmcell_kernel(
             cs = chunk(half, W2)
             if q_ == "s":
                 nc.scalar.activation(
-                    out=gt[2 + hd][:, cs], in_=gt[hd][:, cs], func=ACT.Identity, scale=col(s, 9), bias=col(s, 11)
+                    out=gt[2 + hd][:, cs], in_=gt[hd][:, cs], func=ACT.Identity, scale=sc_(s, 7), bias=sc_(s, 8)
                 )
             else:
                 engine(q_).tensor_scalar(
-                    out=gt[2 + hd][:, cs], in0=gt[hd][:, cs], scalar1=col(s, 9), scalar2=col(s, 11),
+                    out=gt[2 + hd][:, cs], in0=gt[hd][:, cs], scalar1=sc_(s, 7), scalar2=sc_(s, 8),
                     op0=ALU.mult, op1=ALU.add,
                 )
 
@@ -459,9 +502,38 @@ def tile_lstmcell_kernel(
             if ok(t):
                 put("g", ("G1", t), [("r", "H", t, k) for k in range(NQ)], s_g1, ORDER[t])
 
+        def s_S1(t):
+            if ok(t):
+                put("s", ("G1", t), [("r", "H", t, k) for k in range(NQ)], s_s1, ORDER[t])
+
         def s_Q(t):
             if ok(t):
                 put("s", ("Q", t), (("G1", t),), s_q, ORDER[t])
+
+        def s_S2(t):
+            if ok(t):
+                put("s", ("S2", t), (("Q", t), ("g2c",)), s_s2, ORDER[t])
+
+        def s_S5(t):
+            if ok(t):
+                put("s", ("S5", t), (("NA", t),), s_s5, ORDER[t])
+
+        def g_P(t):
+            if ok(t):
+                put("g", ("P", t), (("S2", t), ("S5", t)), s_pow, ORDER[t], 2)
+
+        def s_S6(t):
+            if ok(t):
+                put("s", ("G3", t), (("P", t), ("vc",)), s_s6, ORDER[t])
+
+        def s_C5(hd):
+            put("s", ("C5", hd), (("ca", hd),), s_s5, NJ + hd)
+
+        def g_CP(hd):
+            put("g", ("CP", hd), (("C5", hd),), s_pow, NJ + hd, 1)
+
+        def s_C7(hd):
+            put("s", ("cs", hd), (("CP", hd), ("vc",)), s_s7, hd)
 
         def g_G2(t):
             if ok(t):
@@ -657,22 +729,35 @@ def tile_lstmcell_kernel(
         rd_x(2, 0)
         rd_H("s", 0, 2)
         rd_H("s", 0, 3)
+        s_S1(0)
         rd_x(2, 1)
         rd_x(3, 0)
         s_Q(0)
         rd_x(3, 1)
+        s_S2(0)
         rd_H("s", 1, 2)
         rd_H("s", 1, 3)
+        s_S1(1)
         rd_w(3)
         rd_tb("s", "c", cT, 0)
         s_Q(1)
         rd_H("s", 2, 2)
+        s_S2(1)
         rd_H("s", 2, 3)
+        s_S1(2)
+        s_S5(0)
         rd_tb("s", "c", cT, 1)
+        s_S6(0)
         s_Q(2)
+        s_S5(1)
+        s_S2(2)
         for t in range(NJ):
             for k in range(share(t + LH), NQ):
                 rd_H("s", t + LH, k)
+            s_S1(t + LH)
+            s_S6(t + 1)
+            if t == 6:
+                s_C7(0)
             s_A(t, 0)
             s_A(t, 1)
             if t == 0:
@@ -680,25 +765,25 @@ def tile_lstmcell_kernel(
             if t == 1:
                 rd_tb("s", "c", cT, 3)
                 rd_w(2)
+            if t == 5:
+                s_C5(0)
             s_Q(t + LH)
+            s_S5(t + LN)
+            s_S2(t + LH)
             if t == 6:
                 for k in range(NQ):
                     s_tT(0, k)
                     rd_oc("s", 0, k)
+        s_C5(1)
+        s_C7(1)
         for k in range(NQ):
             s_tT(1, k)
 
         put("g", ("g2c",), (("r", "va"),), s_g2c)
         put("g", ("vc",), (("r", "vb"),), s_vc)
-        g_G1(0)
-        g_G23(-1, 0)
-        g_G1(1)
-        g_G23(0, -1)
-        g_G1(2)
-        g_G23(-1, 1)
+        g_P(0)
+        g_P(1)
         for t in range(NJ):
-            g_G23(t + 1, t + 2)
-            g_G1(t + LH)
             if t < 2:
                 x_fc("g", 0, t)
             if t == 2:
@@ -707,14 +792,15 @@ def tile_lstmcell_kernel(
                 x_ig("g", 0, 1)
             if t == 4:
                 x_fc("g", 1, 0)
+            g_P(t + LN)
+            if t == 4:
                 x_fc("g", 1, 1)
             if t == 5:
-                g_cs(0)
+                g_CP(0)
             if t == 6:
                 x_ig("g", 1, 0)
                 x_ig("g", 1, 1)
-            if t == 7:
-                g_cs(1)
+        g_CP(1)
 
         pe_tb("wh", wh, 0, "hh")
         pe_tb("wh", wh, 1, "hh")

@@ -402,7 +402,7 @@ def tile_lstmcell_kernel(
             engine(q_).tensor_tensor(out=gt[hd][:, cs], in0=gt[hd][:, cs], in1=gt[2 + hd][:, cs], op=ALU.add)
 
         def s_bnc(hd, half):
-            if half == 0:
+            if NJ + hd not in sts:
                 st3 = work.tile([P, NQ, 6], F32, tag="st", bufs=4, name="st3")
                 sts[NJ + hd] = st3
             for k in (2 * half, 2 * half + 1):
@@ -687,27 +687,29 @@ def tile_lstmcell_kernel(
                     v_ca(0)
             if t == 2:
                 v_wq(2)
-            if t == 6:
-                v_cn(0, 0)
-                v_cn(0, 1)
             if t == 7:
-                v_add(1, 0)
+                x_ig("v", 1, 1)
                 v_add(1, 1)
+                v_bnc(1, 0)
                 v_ca(1)
                 for k in range(NQ):
                     rd_ho(0, k)
                 v_cn(1, 0)
                 v_cn(1, 1)
-            for k in range(NQ):
-                v_N(t + LN, k)
+            if t < 5:
+                for k in range(NQ):
+                    v_N(t + LN, k)
             rd_H("v", t + LH + 1, 0)
-            v_NA(t + LN)
+            if t < 5:
+                v_NA(t + LN)
             if share(t + LH + 1) > 1:
                 rd_H("v", t + LH + 1, 1)
-            if t == 3:
-                v_add(0, 0)
             if t == 4:
-                v_add(0, 1)
+                for k in range(NQ):
+                    v_N(7, k)
+                v_bnc(0, 0)
+                v_NA(7)
+                v_bnc(0, 1)
         for k in range(NQ):
             rd_oc("v", 1, k)
             rd_ho(1, k)
@@ -758,6 +760,8 @@ def tile_lstmcell_kernel(
             s_S6(t + 1)
             if t == 6:
                 s_C7(0)
+                x_cn("s", 0, 0)
+                x_cn("s", 0, 1)
             s_A(t, 0)
             s_A(t, 1)
             if t == 0:
@@ -768,14 +772,19 @@ def tile_lstmcell_kernel(
             if t == 5:
                 s_C5(0)
             s_Q(t + LH)
-            s_S5(t + LN)
+            if t < 5:
+                s_S5(t + LN)
             s_S2(t + LH)
+            if t == 4:
+                s_S5(7)
             if t == 6:
                 for k in range(NQ):
                     s_tT(0, k)
                     rd_oc("s", 0, k)
-        s_C5(1)
-        s_C7(1)
+                    if k == 1:
+                        s_C5(1)
+                    if k == 2:
+                        s_C7(1)
         for k in range(NQ):
             s_tT(1, k)
 
@@ -790,16 +799,19 @@ def tile_lstmcell_kernel(
                 x_ig("g", 0, 0)
             if t == 3:
                 x_ig("g", 0, 1)
+                x_add("g", 0, 0)
             if t == 4:
+                x_add("g", 0, 1)
                 x_fc("g", 1, 0)
-            g_P(t + LN)
+            if t < 5:
+                g_P(t + LN)
             if t == 4:
+                g_P(7)
                 x_fc("g", 1, 1)
             if t == 5:
                 g_CP(0)
-            if t == 6:
                 x_ig("g", 1, 0)
-                x_ig("g", 1, 1)
+                x_add("g", 1, 0)
         g_CP(1)
 
         pe_tb("wh", wh, 0, "hh")
@@ -857,20 +869,21 @@ def tile_lstmcell_kernel(
             if t == 7:
                 for k in range(NQ):
                     pe_oc(0, k, "tp")
+                    pe_ho(0, k, "hh")
             if t == 0:
                 pe_tb("c", cr, 2, "tp")
             if t == 1:
                 pe_tb("c", cr, 3, "tp")
                 pe_w(2, "tp")
-            pe_M("N", t + LN, 0)
-            pe_M("N", t + LN, 1)
-            pe_M("N", t + LN, 2)
-            pe_M("N", t + LN, 3)
+            if t < 5:
+                for k in range(NQ):
+                    pe_M("N", t + LN, k)
             pe_H(t + LH + 1, 0)
             if share(t + LH + 1) > 1:
                 pe_H(t + LH + 1, 1)
-        for k in range(NQ):
-            pe_ho(0, k, "hh")
+            if t == 4:
+                for k in range(NQ):
+                    pe_M("N", 7, k)
         for k in range(NQ):
             pe_oc(1, k, "tp")
             pe_ho(1, k, "ih")

@@ -55,8 +55,11 @@ def tile_lstmcell_kernel(
         nc.vector.memset(dm[:], 0.0)
         nc.vector.memset(vrb[:], 0.0)
 
-        sc = keep.tile([P, I], F32, name="sc")
-        nc.sync.dma_start(out=sc[:], in_=x_scale.rearrange("o k -> (o k)").partition_broadcast(P))
+        scrow = keep.tile([P, I], F32, name="scrow")
+        ones = keep.tile([P, P], F32, name="ones")
+        nc.gpsimd.memset(scrow[:], 0.0)
+        nc.gpsimd.memset(ones[:], 1.0)
+        nc.sync.dma_start(out=scrow[0:1, :], in_=x_scale)
         xv = x_bytes.rearrange("(p n) k -> p n k", n=NB)
         xbytes = []
         for q in range(NQ):
@@ -94,6 +97,10 @@ def tile_lstmcell_kernel(
         warm = psum.tile([P, CW], F32, tag="tp", bufs=TP_BUFS, name="warm")
         for i in range(WARM):
             nc.tensor.matmul(out=warm[:], lhsT=identb[:], rhs=zero[:], start=True, stop=True)
+        scp = psum.tile([P, I], F32, tag="tp", bufs=TP_BUFS, name="scp")
+        nc.tensor.matmul(out=scp[:], lhsT=ones[:], rhs=scrow[:], start=True, stop=True)
+        sc = keep.tile([P, I], F32, name="sc")
+        nc.vector.tensor_copy(out=sc[:], in_=scp[:])
         identf = keep.tile([P, P], F32, name="identf")
         make_identity(nc, identf[:])
         expo = keep.tile([P, 24], F32, name="expo")
@@ -301,7 +308,7 @@ def tile_lstmcell_kernel(
             )
 
         def s_q(j):
-            junk = work.tile([P, B], BF16, tag="junk", name="junk")
+            junk = work.tile([P, B], BF16, tag="junk", bufs=1, name="junk")
             nc.scalar.activation(out=junk[:], in_=gt[j][:], func=ACT.Square, bias=sc_(j, 2), accum_out=qy[:, j : j + 1])
 
         def s_g2(j):

from contextlib import ExitStack

import concourse.mybir as mybir
from concourse.masks import make_identity

B, I, H = 2048, 512, 256
EPS = 1e-5
FLOPS = 2 * B * 4 * H * (I + H)

F32 = mybir.dt.float32
BF16 = mybir.dt.bfloat16
U32 = mybir.dt.uint32
U8 = mybir.dt.uint8
FP8 = mybir.dt.float8_e4m3fn
FP8X4 = mybir.dt.float8_e4m3fn_x4
ALU = mybir.AluOpType
ACT = mybir.ActivationFunctionType

P = 128
NB = B // P
NQ = 4
CW = 512
NJ = 8
ORDER = (0, 2, 6, 1, 3, 7, 4, 5)
V_SHARE = (2, 2, 2, 2, 2, 2, 2, 2)
ON_GPSIMD = ("fc0", "ig0", "fc1")
WARM = 6
PLAIN_DUMMIES = 10
R_FILL = 0
IH_BUFS = 3
HH_BUFS = 3
TP_BUFS = 2
AHEAD = 2


def tile_lstmcell_kernel(
    tc, x_bytes, x_scale, c, h, w_ih, w_hh, b, g_ih, b_ih, g_hh, b_hh, g_c, b_c, out_0, out_1
):
    nc = tc.nc
    with ExitStack() as ctx:
        keep = ctx.enter_context(tc.tile_pool(name="keep", bufs=1))
        work = ctx.enter_context(tc.tile_pool(name="work", bufs=2))
        psum = ctx.enter_context(tc.psum_pool(name="psum", bufs=2))
        ctx.enter_context(tc.manual_schedule())

        def chunk(k, width=CW):
            return slice(k * width, (k + 1) * width)

        vra = keep.tile([P, P], BF16, name="vra")
        vrb = keep.tile([P, P], BF16, name="vrb")
        zero = keep.tile([P, CW], BF16, name="zero")
        dm = keep.tile([P, 2], F32, name="dm")
        nc.vector.memset(zero[:], 0.0)
        nc.vector.memset(vra[:], 0.0)
        nc.vector.memset(dm[:], 0.0)
        nc.vector.memset(vrb[:], 0.0)

        scrow = keep.tile([P, I], F32, name="scrow")
        ones = keep.tile([P, P], F32, name="ones")
        nc.gpsimd.memset(scrow[:], 0.0)
        nc.gpsimd.memset(ones[:], 1.0)
        nc.sync.dma_start(out=scrow[0:1, :], in_=x_scale)
        xv = x_bytes.rearrange("(p n) k -> p n k", n=NB)
        xbytes = []
        for q in range(NQ):
            xbt = keep.tile([P, 4, I], U8, name="xbytes%d" % q)
            xbytes.append(xbt)
        nc.sync.dma_start(out=xbytes[0][:], in_=xv[:, 0:4, :])
        wh = keep.tile([P, NJ, H], BF16, name="wh")
        nc.scalar.dma_start(out=wh[:], in_=w_hh.rearrange("(j m) k -> m j k", m=P))
        hr = keep.tile([P, NB, H], BF16, name="hr")
        hv = h.rearrange("(p n) k -> p n k", n=NB)
        nc.scalar.dma_start(out=hr[:, 0:8, :], in_=hv[:, 0:8, :])
        nc.scalar.dma_start(out=vra[0:8, :], in_=g_hh.rearrange("(j m) -> j m", m=P))
        nc.sync.dma_start(out=xbytes[1][:], in_=xv[:, 4:8, :])
        wi = keep.tile([P, NJ, I], BF16, name="wi")
        wiv = w_ih.rearrange("(j m) k -> m j k", m=P)
        nc.sync.dma_start(out=wi[:, 0:4, :], in_=wiv[:, 0:4, :])
        nc.sync.dma_start(out=xbytes[2][:], in_=xv[:, 8:12, :])
        nc.sync.dma_start(out=hr[:, 8:16, :], in_=hv[:, 8:16, :])
        nc.sync.dma_start(out=xbytes[3][:], in_=xv[:, 12:16, :])
        nc.sync.dma_start(out=wi[:, 4:8, :], in_=wiv[:, 4:8, :])
        row = 0
        for vec in (b, g_ih, b_ih, b_hh, g_c, b_c):
            rows = vec.shape[0] // P
            nc.sync.dma_start(out=vrb[row : row + rows, :], in_=vec.rearrange("(j m) -> j m", m=P))
            row += rows
        NV = row
        cr = keep.tile([P, NB, H], BF16, name="cr")
        cv = c.rearrange("(p n) k -> p n k", n=NB)
        for half in range(2):
            nc.sync.dma_start(out=cr[:, 8 * half : 8 * half + 8, :], in_=cv[:, 8 * half : 8 * half + 8, :])

        nc.scalar.activation(out=dm[:, 1:2], in_=dm[:, 0:1], func=ACT.Sigmoid)
        identb = keep.tile([P, P], BF16, name="identb")
        make_identity(nc, identb[:])
        warm = psum.tile([P, CW], F32, tag="tp", bufs=TP_BUFS, name="warm")
        for i in range(WARM):
            nc.tensor.matmul(out=warm[:], lhsT=identb[:], rhs=zero[:], start=True, stop=True)
        scp = psum.tile([P, I], F32, tag="tp", bufs=TP_BUFS, name="scp")
        nc.tensor.matmul(out=scp[:], lhsT=ones[:], rhs=scrow[:], start=True, stop=True)
        sc = keep.tile([P, I], F32, name="sc")
        nc.vector.tensor_copy(out=sc[:], in_=scp[:])
        identf = keep.tile([P, P], F32, name="identf")
        make_identity(nc, identf[:])
        expo = keep.tile([P, 24], F32, name="expo")
        nc.gpsimd.memset(expo[:, 0:8], -1.0)
        nc.gpsimd.memset(expo[:, 8:16], -0.5)
        nc.gpsimd.memset(expo[:, 16:24], 1.0)
        mh = expo[:, 8:9]

        pca = keep.tile([P, 8], F32, name="pca")
        pcb = keep.tile([P, NV], F32, name="pcb")
        v_g2 = pca[:, 0:8]
        v_b, v_g1, v_b1, v_b2 = [pcb[:, 8 * i : 8 * i + 8] for i in range(4)]
        v_gc, v_bc = pcb[:, 32:34], pcb[:, 34:36]
        gc = keep.tile([P, 3, 8], F32, name="gc")
        g2sq, igb, bsum = [gc[:, i, :] for i in range(3)]
        gw = keep.tile([P, NJ + 2, 16], F32, name="gw")
        nc.gpsimd.tensor_tensor(out=gw[:, 0, 15:16], in0=expo[:, 16:17], in1=mh, op=ALU.pow)

        whT = keep.tile([P, 2, NJ * P], BF16, name="whT")
        hT = keep.tile([P, 2, B], BF16, name="hT")
        cT = keep.tile([P, 2, B], BF16, name="cT")
        xq = keep.tile([P, B], U32, name="xq", align_bytes=64)
        xs = keep.tile([P, B], U8, name="xs", align_bytes=64)
        wq = keep.tile([P, NJ * P], U32, name="wq", align_bytes=64)
        ws = keep.tile([P, NJ * P], U8, name="ws", align_bytes=64)
        gt = []
        for j in range(NJ):
            gtile = keep.tile([P, B], F32, name="gt%d" % j)
            gt.append(gtile)
        sy = keep.tile([P, NJ, 4], F32, name="sy")
        qy = keep.tile([P, NJ], F32, name="qy")
        mv = keep.tile([P, NJ + 2, 2], F32, name="mv")
        o0v = out_0.rearrange("(p n) c -> p n c", n=NB)
        o1v = out_1.rearrange("(p n) c -> p n c", n=NB)
        W2 = 2 * CW
        ps, xbs, xgs, wgs, sts, sgs, ths = {}, {}, {}, {}, {}, {}, {}
        SG_BUFS = 16

        def col(j, i):
            return gw[:, j, i : i + 1]

        queues = {"pe": [], "v": [], "s": [], "g": [], "sp": []}
        rings = {"ih": [], "hh": [], "tp": []}
        BUFS = {"ih": IH_BUFS, "hh": HH_BUFS, "tp": TP_BUFS}

        def put(q, name, needs, fn, *args):
            queues[q].append((name, tuple(needs), fn, args))

        def fill(tag, name, needs, fn, *args):
            ring = rings[tag]
            needs = tuple(needs)
            if len(ring) >= BUFS[tag]:
                needs = needs + ring[len(ring) - BUFS[tag]]
            ring.append((("r",) + name, ("tT",) + name[1:]) if name[0] == "oc" else (("r",) + name,))
            put("pe", name, needs, fn, tag, name, *args)

        def engine(q):
            return {"v": nc.vector, "s": nc.scalar, "g": nc.gpsimd}[q]

        def f_tb(tag, name, src, q):
            t = psum.tile([P, 2, 4, P], BF16, tag=tag, bufs=BUFS[tag], name="tb")
            ps[name] = t
            for e in range(2):
                for a in range(4):
                    nc.tensor.transpose(t[:, e, a, :], src[:, 4 * q + a, e * P : (e + 1) * P], identb[:])

        def r_tb(q_, name, dst, q):
            src = ps[name][:].rearrange("k e a m -> k e (a m)")
            if q_ == "v":
                nc.vector.tensor_copy(out=dst[:, :, chunk(q)], in_=src)
            else:
                nc.scalar.copy(out=dst[:, :, chunk(q)], in_=src)

        def f_vec(tag, name, src):
            t = psum.tile([P, P], BF16, tag=tag, bufs=BUFS[tag], name="pcp")
            ps[name] = t
            nc.tensor.transpose(t[:], src[:], identb[:])

        def r_vec(name, dst, n):
            nc.scalar.copy(out=dst[:], in_=ps[name][:, 0:n])

        def f_tw(tag, name, rows):
            t = psum.tile([P, 2, 2, P], F32, tag=tag, bufs=BUFS[tag], name="tw")
            ps[name] = t
            for a in range(2):
                words = rows(a).bitcast(F32)
                for u in range(2):
                    nc.tensor.transpose(t[:, a, u, :], words[:, u : I // 2 : 2], identf[:])

        def r_tw(name, dst):
            nc.scalar.copy(out=dst(), in_=ps[name][:].rearrange("k a u m -> k a m u"))

        def s_xp(q, a):
            if a == 0:
                xb = work.tile([P, 4, I], BF16, tag="xb", bufs=4, name="xb")
                xbs[q] = xb
            nc.vector.tensor_tensor(out=xbs[q][:, a, :], in0=xbytes[q][:, a, :].bitcast(FP8), in1=sc[:], op=ALU.mult)

        def x_dst(q, half):
            if half == 0:
                xg = work.tile([P, CW, 4], BF16, tag="xg", bufs=4, name="xg", align_bytes=64)
                xgs[q] = xg
            v = xgs[q][:].rearrange("k c t -> k (c t)").bitcast(F32).rearrange("k (a m u) -> k a m u", a=4, u=2)
            return v[:, 2 * half : 2 * half + 2, :, :]

        def w_dst(pr):
            wg = work.tile([P, 2 * P, 4], BF16, tag="wg", bufs=4, name="wg", align_bytes=64)
            wgs[pr] = wg
            return wg[:].rearrange("k c t -> k (c t)").bitcast(F32).rearrange("k (a m u) -> k a m u", a=2, u=2)

        def s_xq(q):
            nc.vector.quantize_mx(
                out=xq[:, chunk(q)].bitcast(FP8X4), scales=xs[:, chunk(q)], in_=xgs[q][:].rearrange("k c t -> k (c t)")
            )

        def s_wq(pr):
            cols = slice(pr * 2 * P, (pr + 1) * 2 * P)
            nc.vector.quantize_mx(
                out=wq[:, cols].bitcast(FP8X4), scales=ws[:, cols], in_=wgs[pr][:].rearrange("k c t -> k (c t)")
            )

        def s_g2c():
            nc.gpsimd.tensor_tensor(out=g2sq, in0=v_g2, in1=v_g2, op=ALU.mult)
            nc.gpsimd.tensor_scalar(out=g2sq, in0=g2sq, scalar1=1e-30, scalar2=float(B), op0=ALU.max, op1=ALU.mult)
            nc.gpsimd.tensor_tensor(out=igb, in0=g2sq, in1=expo[:, 0:8], op=ALU.pow)

        def s_vc():
            nc.gpsimd.tensor_tensor(out=bsum, in0=v_b, in1=v_b1, op=ALU.add)
            nc.gpsimd.tensor_tensor(out=bsum, in0=bsum, in1=v_b2, op=ALU.add)
            nc.gpsimd.tensor_scalar(out=gw[:, 0:NJ, 7], in0=v_g1, scalar1=-1.0, scalar2=0.0, op0=ALU.mult, op1=ALU.add)
            nc.gpsimd.tensor_scalar(
                out=gw[:, NJ : NJ + 2, 6], in0=v_gc, scalar1=1.0, scalar2=0.0, op0=ALU.mult, op1=ALU.add
            )
            nc.gpsimd.tensor_scalar(
                out=gw[:, NJ : NJ + 2, 7], in0=v_gc, scalar1=-1.0, scalar2=0.0, op0=ALU.mult, op1=ALU.add
            )

        def f_hh(tag, name, j, k):
            t = psum.tile([P, CW], F32, tag=tag, bufs=BUFS[tag], name="hp")
            ps[name] = t
            for e in range(2):
                nc.tensor.matmul(
                    out=t[:], lhsT=whT[:, e, j * P : (j + 1) * P], rhs=hT[:, e, chunk(k)], start=(e == 0), stop=(e == 1)
                )

        def r_hh(q_, name, j, k):
            if q_ == "v":
                nc.vector.tensor_scalar(
                    out=gt[j][:, chunk(k)], in0=ps[name][:], scalar1=v_g2[:, j : j + 1], scalar2=None,
                    op0=ALU.mult, op1=ALU.add, accum_out=sy[:, j, k : k + 1],
                )
            else:
                nc.scalar.activation(
                    out=gt[j][:, chunk(k)], in_=ps[name][:], func=ACT.Identity, scale=v_g2[:, j : j + 1],
                    accum_out=sy[:, j, k : k + 1],
                )

        sw = keep.tile([P, NJ + 2, 16], F32, name="sw")
        rr = keep.tile([P, NJ + 2, 2], F32, name="rr")
        epst = keep.tile([P, 1], F32, name="epst")
        nc.gpsimd.memset(epst[:], EPS)

        def sc_(slot, i):
            return sw[:, slot, i : i + 1]

        def fma(out, in_, scale, bias=None):
            if bias is None:
                nc.scalar.activation(out=out, in_=in_, func=ACT.Identity, scale=scale)
            else:
                nc.scalar.activation(out=out, in_=in_, func=ACT.Identity, scale=scale, bias=bias)

        def s_s1(j):
            nc.scalar.activation(
                out=sw[:, j, 9:13], in_=sy[:, j, :], func=ACT.Identity, scale=-1.0 / B, accum_out=sc_(j, 2)
            )

        def s_s2(j):
            fma(sc_(j, 1), qy[:, j : j + 1], igb[:, j : j + 1], epst[:])

        def s_s5(slot):
            fma(sc_(slot, 0), mv[:, slot, 1:2], 1.0, epst[:])

        def s_pow(slot, n):
            nc.gpsimd.tensor_tensor(out=rr[:, slot, 0:n], in0=sw[:, slot, 0:n], in1=expo[:, 8 : 8 + n], op=ALU.pow)

        def s_s6(j):
            r1, r2 = rr[:, j, 0:1], rr[:, j, 1:2]
            fma(sc_(j, 3), sc_(j, 1), r2)
            fma(sc_(j, 5), r1, v_g1[:, j : j + 1])
            fma(sc_(j, 6), r1, col(j, 7))
            fma(sc_(j, 4), sc_(j, 2), r2, bsum[:, j : j + 1])
            fma(sc_(j, 7), sc_(j, 3), sc_(j, 5))
            fma(sc_(j, 8), mv[:, j, 0:1], sc_(j, 6), sc_(j, 4))

        def s_s7(hd):
            s = NJ + hd
            fma(sc_(s, 7), rr[:, s, 0:1], v_gc[:, hd : hd + 1])
            fma(sc_(s, 6), rr[:, s, 0:1], col(s, 7))
            fma(sc_(s, 8), mv[:, s, 0:1], sc_(s, 6), v_bc[:, hd : hd + 1])

        def s_g1(j):
            nc.gpsimd.tensor_tensor(out=gw[:, j, 0:2], in0=sy[:, j, 0:2], in1=sy[:, j, 2:4], op=ALU.add)
            nc.gpsimd.tensor_scalar(
                out=col(j, 2), in0=col(j, 0), scalar1=col(j, 1), scalar2=-1.0 / B, op0=ALU.add, op1=ALU.mult
            )

        def s_q(j):
            junk = work.tile([P, B], BF16, tag="junk", bufs=1, name="junk")
            nc.scalar.activation(out=junk[:], in_=gt[j][:], func=ACT.Square, bias=sc_(j, 2), accum_out=qy[:, j : j + 1])

        def s_g2(j):
            nc.gpsimd.tensor_scalar(
                out=col(j, 3), in0=qy[:, j : j + 1], scalar1=igb[:, j : j + 1], scalar2=EPS, op0=ALU.mult, op1=ALU.add
            )
            nc.gpsimd.tensor_tensor(out=col(j, 4), in0=col(j, 3), in1=mh, op=ALU.pow)
            nc.gpsimd.tensor_scalar(
                out=col(j, 6), in0=col(j, 3), scalar1=col(j, 4), scalar2=v_g1[:, j : j + 1], op0=ALU.mult, op1=ALU.mult
            )
            nc.gpsimd.tensor_scalar(
                out=col(j, 12), in0=col(j, 2), scalar1=col(j, 4), scalar2=bsum[:, j : j + 1], op0=ALU.mult, op1=ALU.add
            )

        def s_norm(slot, beta):
            nc.gpsimd.tensor_scalar(
                out=col(slot, 5), in0=mv[:, slot, 1:2], scalar1=1.0, scalar2=EPS, op0=ALU.mult, op1=ALU.add
            )
            nc.gpsimd.tensor_tensor(out=col(slot, 8), in0=col(slot, 5), in1=mh, op=ALU.pow)
            nc.gpsimd.tensor_scalar(
                out=gw[:, slot, 9:11], in0=gw[:, slot, 6:8], scalar1=col(slot, 8), scalar2=0.0, op0=ALU.mult, op1=ALU.add
            )
            nc.gpsimd.tensor_scalar(
                out=col(slot, 11), in0=mv[:, slot, 0:1], scalar1=col(slot, 10), scalar2=beta, op0=ALU.mult, op1=ALU.add
            )

        def s_g23(ja, jb):
            if jb is not None:
                nc.gpsimd.tensor_scalar(
                    out=col(jb, 3), in0=qy[:, jb : jb + 1], scalar1=igb[:, jb : jb + 1], scalar2=EPS, op0=ALU.mult, op1=ALU.add
                )
            if ja is not None:
                nc.gpsimd.tensor_scalar(
                    out=col(ja, 5), in0=mv[:, ja, 1:2], scalar1=1.0, scalar2=EPS, op0=ALU.mult, op1=ALU.add
                )
            if jb is not None:
                nc.gpsimd.tensor_tensor(out=col(jb, 4), in0=col(jb, 3), in1=mh, op=ALU.pow)
            if ja is not None:
                nc.gpsimd.tensor_tensor(out=col(ja, 8), in0=col(ja, 5), in1=mh, op=ALU.pow)
            if jb is not None:
                nc.gpsimd.tensor_scalar(
                    out=col(jb, 6), in0=col(jb, 3), scalar1=col(jb, 4), scalar2=v_g1[:, jb : jb + 1], op0=ALU.mult, op1=ALU.mult
                )
            if ja is not None:
                nc.gpsimd.tensor_scalar(
                    out=gw[:, ja, 9:11], in0=gw[:, ja, 6:8], scalar1=col(ja, 8), scalar2=0.0, op0=ALU.mult, op1=ALU.add
                )
            if jb is not None:
                nc.gpsimd.tensor_scalar(
                    out=col(jb, 12), in0=col(jb, 2), scalar1=col(jb, 4), scalar2=bsum[:, jb : jb + 1], op0=ALU.mult, op1=ALU.add
                )
            if ja is not None:
                nc.gpsimd.tensor_scalar(
                    out=col(ja, 11), in0=mv[:, ja, 0:1], scalar1=col(ja, 10), scalar2=col(ja, 12), op0=ALU.mult, op1=ALU.add
                )

        def f_mx(tag, name, j, k):
            t = psum.tile([P, CW], F32, tag=tag, bufs=BUFS[tag], name="ip")
            ps[name] = t
            nc.tensor.matmul_mx(
                out=t[:],
                lhsT=wq[:, j * P : (j + 1) * P].bitcast(FP8X4), lhsT_scale=ws[:, j * P : (j + 1) * P],
                rhs=xq[:, chunk(k)].bitcast(FP8X4), rhs_scale=xs[:, chunk(k)],
                start=True, stop=True,
            )

        def r_bn(name, j, k):
            if k == 0:
                st = work.tile([P, NQ, 6], F32, tag="st", bufs=4, name="st")
                sts[j] = st
            nc.vector.bn_stats(out=sts[j][:, k, :], in_=ps[name][:])

        def s_aggr(slot, key):
            nc.vector.bn_aggr(out=mv[:, slot, :], in_=sts[key][:].rearrange("p a s -> p (a s)"))

        def r_join(name, j, k):
            nc.vector.scalar_tensor_tensor(
                out=gt[j][:, chunk(k)], in0=ps[name][:], scalar=sc_(j, 7), in1=gt[j][:, chunk(k)],
                op0=ALU.mult, op1=ALU.add,
            )

        def s_act(j, half):
            nc.scalar.activation(
                out=gt[j][:, chunk(half, W2)], in_=gt[j][:, chunk(half, W2)],
                func=(ACT.Tanh if j >= 6 else ACT.Sigmoid), scale=rr[:, j, 1:2], bias=sc_(j, 8),
            )

        def s_fc(q_, hd, half):
            cs = chunk(half, W2)
            engine(q_).tensor_tensor(out=gt[hd][:, cs], in0=gt[hd][:, cs], in1=cT[:, hd, cs], op=ALU.mult)

        def s_ig(q_, hd, half):
            cs = chunk(half, W2)
            engine(q_).tensor_tensor(out=gt[2 + hd][:, cs], in0=gt[2 + hd][:, cs], in1=gt[6 + hd][:, cs], op=ALU.mult)

        def s_add(q_, hd, half):
            cs = chunk(half, W2)
            engine(q_).tensor_tensor(out=gt[hd][:, cs], in0=gt[hd][:, cs], in1=gt[2 + hd][:, cs], op=ALU.add)

        def s_bnc(hd, half):
            if NJ + hd not in sts:
                st3 = work.tile([P, NQ, 6], F32, tag="st", bufs=4, name="st3")
                sts[NJ + hd] = st3
            for k in (2 * half, 2 * half + 1):
                nc.vector.bn_stats(out=sts[NJ + hd][:, k, :], in_=gt[hd][:, chunk(k)])

        def s_cn(q_, hd, half):
            s = NJ + hd
            cs = chunk(half, W2)
            if q_ == "s":
                nc.scalar.activation(
                    out=gt[2 + hd][:, cs], in_=gt[hd][:, cs], func=ACT.Identity, scale=sc_(s, 7), bias=sc_(s, 8)
                )
            else:
                engine(q_).tensor_scalar(
                    out=gt[2 + hd][:, cs], in0=gt[hd][:, cs], scalar1=sc_(s, 7), scalar2=sc_(s, 8),
                    op0=ALU.mult, op1=ALU.add,
                )

        def s_tanh(name):
            th = work.tile([P, 4, P], F32, tag="th", bufs=8, name="th")
            ths[name] = th
            nc.scalar.activation(out=th[:], in_=ps[name][:], func=ACT.Tanh)

        def r_prod(name, cname):
            sg = work.tile([P, 4, P], F32, tag="sg", bufs=SG_BUFS, name="sg")
            sgs[name] = sg
            nc.vector.tensor_tensor(out=sg[:], in0=ps[name][:], in1=ths[cname][:], op=ALU.mult)

        def f_out(tag, name, src, k):
            t = psum.tile([P, 4, P], F32, tag=tag, bufs=BUFS[tag], name="pt")
            ps[name] = t
            for a in range(4):
                nc.tensor.transpose(t[:, a, :], src[:, k * CW + a * P : k * CW + (a + 1) * P], identf[:])

        def r_out(q_, name):
            sg = work.tile([P, 4, P], F32, tag="sg", bufs=SG_BUFS, name="sg")
            sgs[name] = sg
            if q_ == "v":
                nc.vector.tensor_copy(out=sg[:], in_=ps[name][:])
            else:
                nc.scalar.copy(out=sg[:], in_=ps[name][:])

        def s_store(name, k, hd, outv):
            nc.sync.dma_start(out=outv[:, 4 * k : 4 * k + 4, hd * P : (hd + 1) * P], in_=sgs[name][:])

        T_OF = {}
        for t in range(NJ):
            T_OF[ORDER[t]] = t

        def ok(t):
            return 0 <= t < NJ

        def pe_tb(what, src, q, tag):
            fill(tag, (what, q), (), f_tb, src, q)

        def rd_tb(q_, what, dst, q):
            put(q_, ("r", what, q), ((what, q),), r_tb, q_, (what, q), dst, q)

        def pe_vec(what, src):
            fill("tp", (what,), (), f_vec, src)

        def rd_vec(what, dst, n):
            put("s", ("r", what), ((what,),), r_vec, (what,), dst, n)

        def v_xp(q, parts):
            for a in parts:
                put("v", ("xp", q, a), (), s_xp, q, a)

        def pe_x(q, half):
            fill("ih", ("x", q, half), (("xp", q, 2 * half), ("xp", q, 2 * half + 1)), f_tw,
                 lambda a: xbs[q][:, 2 * half + a, :])

        def rd_x(q, half):
            put("s", ("r", "x", q, half), (("x", q, half),), r_tw, ("x", q, half), lambda: x_dst(q, half))

        def pe_w(pr, tag):
            fill(tag, ("w", pr), (), f_tw, lambda a: wi[:, 2 * pr + a, :])

        def rd_w(pr):
            put("s", ("r", "w", pr), (("w", pr),), r_tw, ("w", pr), lambda: w_dst(pr))

        def v_xq(q):
            put("v", ("xq", q), (("r", "x", q, 0), ("r", "x", q, 1)), s_xq, q)

        def v_wq(pr):
            put("v", ("wq", pr), (("r", "w", pr),), s_wq, pr)

        def pe_H(t, k):
            if ok(t):
                fill("hh", ("H", t, k), (("r", "wh", ORDER[t] // 4), ("r", "h", k)), f_hh, ORDER[t], k)

        def rd_H(q_, t, k):
            if ok(t):
                put(q_, ("r", "H", t, k), (("H", t, k), ("r", "va")), r_hh, q_, ("H", t, k), ORDER[t], k)

        def g_G1(t):
            if ok(t):
                put("g", ("G1", t), [("r", "H", t, k) for k in range(NQ)], s_g1, ORDER[t])

        def s_S1(t):
            if ok(t):
                put("s", ("G1", t), [("r", "H", t, k) for k in range(NQ)], s_s1, ORDER[t])

        def s_Q(t):
            if ok(t):
                put("s", ("Q", t), (("G1", t),), s_q, ORDER[t])

        def s_S2(t):
            if ok(t):
                put("s", ("S2", t), (("Q", t), ("g2c",)), s_s2, ORDER[t])

        def s_S5(t):
            if ok(t):
                put("s", ("S5", t), (("NA", t),), s_s5, ORDER[t])

        def g_P(t):
            if ok(t):
                put("g", ("P", t), (("S2", t), ("S5", t)), s_pow, ORDER[t], 2)

        def s_S6(t):
            if ok(t):
                put("s", ("G3", t), (("P", t), ("vc",)), s_s6, ORDER[t])

        def s_C5(hd):
            put("s", ("C5", hd), (("ca", hd),), s_s5, NJ + hd)

        def g_CP(hd):
            put("g", ("CP", hd), (("C5", hd),), s_pow, NJ + hd, 1)

        def s_C7(hd):
            put("s", ("cs", hd), (("CP", hd), ("vc",)), s_s7, hd)

        def g_G2(t):
            if ok(t):
                put("g", ("G2", t), (("Q", t), ("g2c",), ("vc",)), s_g2, ORDER[t])

        def g_G23(ta, tb):
            needs = [("g2c",), ("vc",)]
            if ok(ta):
                needs += [("NA", ta), ("G2", ta)]
            if ok(tb):
                needs += [("Q", tb)]
            if ok(ta) or ok(tb):
                put("g", ("G23", ta, tb), needs, s_g23, ORDER[ta] if ok(ta) else None, ORDER[tb] if ok(tb) else None)

        def pe_M(stage, t, k):
            if ok(t):
                fill("ih", (stage, t, k), (("wq", ORDER[t] // 2), ("xq", k)), f_mx, ORDER[t], k)

        def v_N(t, k):
            if ok(t):
                put("v", ("r", "N", t, k), (("N", t, k),), r_bn, ("N", t, k), ORDER[t], k)

        def v_NA(t):
            if ok(t):
                put("v", ("NA", t), [("r", "N", t, k) for k in range(NQ)], s_aggr, ORDER[t], ORDER[t])

        def g_G3(t):
            if ok(t):
                put("g", ("G3", t), (("NA", t), ("G2", t)), s_norm, ORDER[t], col(ORDER[t], 12))

        def v_J(t, k):
            if ok(t):
                put("v", ("r", "J", t, k), (("J", t, k), ("G3", t), ("Q", t), ("r", "H", t, k)), r_join,
                    ("J", t, k), ORDER[t], k)

        def s_A(t, half):
            if ok(t):
                put("s", ("A", t, half), (("r", "J", t, 2 * half), ("r", "J", t, 2 * half + 1)), s_act, ORDER[t], half)

        def x_fc(q_, hd, half):
            put(q_, ("fc", hd, half), (("A", T_OF[hd], half), ("r", "c", 2 * half), ("r", "c", 2 * half + 1)),
                s_fc, q_, hd, half)

        def x_ig(q_, hd, half):
            put(q_, ("ig", hd, half), (("A", T_OF[2 + hd], half), ("A", T_OF[6 + hd], half)), s_ig, q_, hd, half)

        def x_add(q_, hd, half):
            put(q_, ("add", hd, half), (("fc", hd, half), ("ig", hd, half)), s_add, q_, hd, half)

        def v_bnc(hd, half):
            put("v", ("bnc", hd, half), (("add", hd, half),), s_bnc, hd, half)

        def v_add(hd, half):
            x_add("v", hd, half)
            v_bnc(hd, half)

        def v_ca(hd):
            put("v", ("ca", hd), (("bnc", hd, 0), ("bnc", hd, 1)), s_aggr, NJ + hd, NJ + hd)

        def g_cs(hd):
            put("g", ("cs", hd), (("ca", hd), ("vc",)), s_norm, NJ + hd, v_bc[:, hd : hd + 1])

        def x_cn(q_, hd, half):
            put(q_, ("cn", hd, half), (("cs", hd),), s_cn, q_, hd, half)

        def v_cn(hd, half):
            x_cn("v", hd, half)

        def s_tT(hd, k):
            put("s", ("tT", hd, k), (("oc", hd, k),), s_tanh, ("oc", hd, k))

        def pe_oc(hd, k, tag):
            fill(tag, ("oc", hd, k), (("cn", hd, k // 2),), f_out, gt[2 + hd], k)

        def rd_oc(q_, hd, k):
            put(q_, ("r", "oc", hd, k), (("oc", hd, k), ("tT", hd, k)), r_out, q_, ("oc", hd, k))

        def st_oc(hd, k):
            put("sp", ("st", "oc", hd, k), (("r", "oc", hd, k),), s_store, ("oc", hd, k), k, hd, o0v)

        def pe_ho(hd, k, tag):
            fill(tag, ("ho", hd, k), (("A", T_OF[4 + hd], k // 2),), f_out, gt[4 + hd], k)

        def rd_ho(hd, k):
            put("v", ("r", "ho", hd, k), (("ho", hd, k), ("tT", hd, k)), r_prod, ("ho", hd, k), ("oc", hd, k))

        def st_ho(hd, k):
            put("sp", ("st", "ho", hd, k), (("r", "ho", hd, k),), s_store, ("ho", hd, k), k, hd, o1v)

        def run():
            done = set()
            pos = {"pe": 0, "v": 0, "s": 0, "g": 0, "sp": 0}
            left = sum(len(queues[q]) for q in pos)
            while left > 0:
                moved = 0
                for q in ("pe", "v", "s", "g", "sp"):
                    lst = queues[q]
                    while pos[q] < len(lst) and all(n in done for n in lst[pos[q]][1]):
                        name, needs, fn, args = lst[pos[q]]
                        fn(*args)
                        done.add(name)
                        if name[0] == "G23":
                            done.add(("G3", name[1]))
                            done.add(("G2", name[2]))
                        pos[q] += 1
                        moved += 1
                assert moved > 0, [queues[q][pos[q]][0:2] for q in pos if pos[q] < len(queues[q])]
                left -= moved

        LH = 3
        LN = 2

        def share(t):
            return V_SHARE[t] if ok(t) else 2

        v_xp(0, (0, 1, 2, 3))
        v_xp(1, (0, 1, 2, 3))
        v_xp(2, (0,))
        rd_H("v", 0, 0)
        v_xp(2, (1, 2, 3))
        v_xp(3, (0,))
        rd_H("v", 0, 1)
        v_xp(3, (1, 2, 3))
        v_wq(0)
        v_wq(1)
        v_xq(0)
        v_xq(1)
        rd_H("v", 1, 0)
        v_xq(2)
        rd_H("v", 1, 1)
        v_N(0, 0)
        v_N(0, 1)
        rd_H("v", 2, 0)
        v_N(0, 2)
        v_xq(3)
        v_N(1, 0)
        v_N(1, 1)
        v_N(1, 2)
        v_N(0, 3)
        v_wq(3)
        v_NA(0)
        v_N(1, 3)
        rd_H("v", 2, 1)
        v_NA(1)
        rd_H("v", 3, 0)
        rd_H("v", 3, 1)
        for t in range(NJ):
            for k in range(NQ):
                v_J(t, k)
                if t == 5 and k == 0:
                    v_ca(0)
            if t == 2:
                v_wq(2)
            if t == 7:
                x_ig("v", 1, 1)
                v_add(1, 1)
                v_bnc(1, 0)
                v_ca(1)
                for k in range(NQ):
                    rd_ho(0, k)
                v_cn(1, 0)
                v_cn(1, 1)
            if t < 5:
                for k in range(NQ):
                    v_N(t + LN, k)
            rd_H("v", t + LH + 1, 0)
            if t < 5:
                v_NA(t + LN)
            if share(t + LH + 1) > 1:
                rd_H("v", t + LH + 1, 1)
            if t == 4:
                for k in range(NQ):
                    v_N(7, k)
                v_bnc(0, 0)
                v_NA(7)
                v_bnc(0, 1)
        for k in range(NQ):
            rd_oc("v", 1, k)
            rd_ho(1, k)

        rd_tb("s", "wh", whT, 0)
        rd_tb("s", "wh", whT, 1)
        rd_tb("s", "h", hT, 0)
        rd_tb("s", "h", hT, 1)
        rd_x(0, 0)
        rd_x(0, 1)
        rd_vec("va", pca, 8)
        rd_w(0)
        rd_tb("s", "h", hT, 2)
        rd_vec("vb", pcb, NV)
        rd_x(1, 0)
        rd_tb("s", "h", hT, 3)
        rd_x(1, 1)
        rd_w(1)
        rd_x(2, 0)
        rd_H("s", 0, 2)
        rd_H("s", 0, 3)
        s_S1(0)
        rd_x(2, 1)
        rd_x(3, 0)
        s_Q(0)
        rd_x(3, 1)
        s_S2(0)
        rd_H("s", 1, 2)
        rd_H("s", 1, 3)
        s_S1(1)
        rd_w(3)
        rd_tb("s", "c", cT, 0)
        s_Q(1)
        rd_H("s", 2, 2)
        s_S2(1)
        rd_H("s", 2, 3)
        s_S1(2)
        s_S5(0)
        rd_tb("s", "c", cT, 1)
        s_S6(0)
        s_Q(2)
        s_S5(1)
        s_S2(2)
        for t in range(NJ):
            for k in range(share(t + LH), NQ):
                rd_H("s", t + LH, k)
            s_S1(t + LH)
            s_S6(t + 1)
            if t == 6:
                s_C7(0)
                x_cn("s", 0, 0)
                x_cn("s", 0, 1)
            s_A(t, 0)
            s_A(t, 1)
            if t == 0:
                rd_tb("s", "c", cT, 2)
            if t == 1:
                rd_tb("s", "c", cT, 3)
                rd_w(2)
            if t == 5:
                s_C5(0)
            s_Q(t + LH)
            if t < 5:
                s_S5(t + LN)
            s_S2(t + LH)
            if t == 4:
                s_S5(7)
            if t == 6:
                for k in range(NQ):
                    s_tT(0, k)
                    rd_oc("s", 0, k)
                    if k == 1:
                        s_C5(1)
                    if k == 2:
                        s_C7(1)
        for k in range(NQ):
            s_tT(1, k)

        put("g", ("g2c",), (("r", "va"),), s_g2c)
        put("g", ("vc",), (("r", "vb"),), s_vc)
        g_P(0)
        g_P(1)
        for t in range(NJ):
            if t < 2:
                x_fc("g", 0, t)
            if t == 2:
                x_ig("g", 0, 0)
            if t == 3:
                x_ig("g", 0, 1)
                x_add("g", 0, 0)
            if t == 4:
                x_add("g", 0, 1)
                x_fc("g", 1, 0)
            if t < 5:
                g_P(t + LN)
            if t == 4:
                g_P(7)
                x_fc("g", 1, 1)
            if t == 5:
                g_CP(0)
                x_ig("g", 1, 0)
                x_add("g", 1, 0)
        g_CP(1)

        pe_tb("wh", wh, 0, "hh")
        pe_tb("wh", wh, 1, "hh")
        pe_tb("h", hr, 0, "hh")
        pe_tb("h", hr, 1, "hh")
        pe_x(0, 0)
        pe_w(0, "ih")
        pe_x(0, 1)
        pe_vec("va", vra)
        pe_H(0, 0)
        pe_tb("h", hr, 2, "hh")
        pe_x(1, 0)
        pe_x(1, 1)
        pe_vec("vb", vrb)
        pe_w(1, "ih")
        pe_tb("h", hr, 3, "hh")
        pe_H(0, 1)
        pe_x(2, 0)
        pe_w(3, "tp")
        pe_tb("c", cr, 0, "tp")
        pe_H(0, 2)
        pe_H(0, 3)
        pe_x(2, 1)
        pe_x(3, 0)
        pe_H(1, 0)
        pe_H(1, 1)
        pe_x(3, 1)
        pe_H(1, 2)
        pe_M("N", 0, 0)
        pe_H(1, 3)
        pe_M("N", 0, 1)
        pe_H(2, 0)
        pe_M("N", 0, 2)
        pe_M("N", 1, 0)
        pe_M("N", 1, 1)
        pe_H(2, 2)
        pe_M("N", 1, 2)
        pe_H(2, 3)
        pe_M("N", 0, 3)
        pe_tb("c", cr, 1, "tp")
        pe_M("N", 1, 3)
        pe_H(2, 1)
        pe_H(3, 0)
        pe_H(3, 1)
        for t in range(NJ):
            if share(t + LH) < 2:
                pe_H(t + LH, 1)
            pe_H(t + LH, 2)
            pe_M("J", t, 0)
            pe_H(t + LH, 3)
            pe_M("J", t, 1)
            pe_M("J", t, 2)
            pe_M("J", t, 3)
            if t == 7:
                for k in range(NQ):
                    pe_oc(0, k, "tp")
                    pe_ho(0, k, "hh")
            if t == 0:
                pe_tb("c", cr, 2, "tp")
            if t == 1:
                pe_tb("c", cr, 3, "tp")
                pe_w(2, "tp")
            if t < 5:
                for k in range(NQ):
                    pe_M("N", t + LN, k)
            pe_H(t + LH + 1, 0)
            if share(t + LH + 1) > 1:
                pe_H(t + LH + 1, 1)
            if t == 4:
                for k in range(NQ):
                    pe_M("N", 7, k)
        for k in range(NQ):
            pe_oc(1, k, "tp")
            pe_ho(1, k, "ih")

        for k in range(NQ):
            st_oc(0, k)
        for k in range(NQ):
            st_ho(0, k)
        for k in range(NQ):
            st_oc(1, k)
            st_ho(1, k)
        run()
